import numpy as np
import ml_dtypes


def mxq(x, axis, fmt="e4m3"):
    dtype, down = {"e4m3": (ml_dtypes.float8_e4m3fn, 7), "e5m2": (ml_dtypes.float8_e5m2, 14)}[fmt]
    v = np.moveaxis(np.asarray(x, np.float32).astype(ml_dtypes.bfloat16).astype(np.float64), axis, -1)
    blocks = v.reshape(v.shape[:-1] + (-1, 32))
    amax = np.abs(blocks).max(-1, keepdims=True)
    byte = np.maximum(np.where(amax > 0, np.frexp(amax)[1] - 1 + 127, 0) - down, 1)
    scale = np.exp2(byte - 127.0)
    codes = (blocks / scale).astype(np.float32).astype(dtype).astype(np.float64)
    return np.moveaxis((codes * scale).reshape(v.shape), -1, axis)


WIDE = False


def mx_kscale(k):
    if not WIDE:
        return np.ones(k)
    levels = np.array([10, -10, 5, -5, 0])
    if k % 512:
        return np.exp2(np.random.permutation(np.resize(levels, k // 32))).repeat(32)
    a = np.empty((k // 512, 16))
    for p in range(k // 512):
        a[p, :8] = np.random.permutation(np.resize(levels, 8))
        for g in range(8):
            far = levels[np.abs(levels - a[p, g]) >= 10]
            a[p, g + 8] = far[np.random.randint(len(far))]
    return np.exp2(a.ravel()).repeat(32)


BF16 = ml_dtypes.bfloat16


def bf(x):
    return np.asarray(x, np.float32).astype(BF16)


def f64(x):
    return np.asarray(x).astype(np.float64)


B, H, W, NP, C, CO = 16, 8, 9, 9, 512, 512
SHIFTS = ((0, 0), (0, 0), (0, 0), (0, -1), (0, 1), (1, -1), (1, 1), (-1, -1), (-1, 1))


def setup_inputs():
    s = mx_kscale(C)
    t = mx_kscale(NP * CO)
    return {
        "xa": bf(np.random.standard_normal((B, C, H, W)) * 0.65 * s[None, :, None, None]),
        "W9": bf(np.random.standard_normal((NP, CO, C)) / np.sqrt(C) * t.reshape(NP, CO, 1) / s[None, None, :]),
        "b9": bf(np.random.standard_normal((NP, CO)) * 0.3 * t.reshape(NP, CO)),
        "Wf": bf(np.random.standard_normal((C, NP * CO)) / np.sqrt(NP * CO) / t[None, :]),
        "b_fuse": bf(np.random.standard_normal(C) * 0.3),
    }


def reference(xa, W9, b9, Wf, b_fuse):
    y = mxq(f64(W9).reshape(NP * CO, C), 1, "e4m3") @ mxq(f64(xa).reshape(B, C, H * W), 1, "e4m3")
    y = (y + f64(b9).reshape(NP * CO)[None, :, None]).reshape(B, NP, CO, H, W)
    out = np.zeros((B, C, H, W)) + f64(b_fuse)[None, :, None, None]
    for k, (dh, dw) in enumerate(SHIFTS):
        hn, wn = H - abs(dh), W - abs(dw)
        hs, ws = max(dh, 0), max(dw, 0)
        hd, wd = max(-dh, 0), max(-dw, 0)
        src = y[:, k, :, hs:hs + hn, ws:ws + wn].reshape(B, CO, hn * wn)
        p = mxq(f64(Wf)[:, k * CO:(k + 1) * CO], 1, "e4m3") @ mxq(src, 1, "e4m3")
        out[:, :, hd:hd + hn, wd:wd + wn] += p.reshape(B, C, hn, wn)
    return out

@@ -1,0 +1,342 @@
+from contextlib import ExitStack
+
+import concourse.mybir as mybir
+from concourse.masks import make_identity
+
+F32 = mybir.dt.float32
+BF16 = mybir.dt.bfloat16
+U32 = mybir.dt.uint32
+U8 = mybir.dt.uint8
+FP8X4 = mybir.dt.float8_e4m3fn_x4
+IDENTITY = mybir.ActivationFunctionType.Identity
+ADD = mybir.AluOpType.add
+
+B, C, H, W, NP, CO = 16, 512, 8, 9, 9, 512
+SHIFTS = ((0, 0), (0, 0), (0, 0), (0, -1), (0, 1), (1, -1), (1, 1), (-1, -1), (-1, 1))
+USED = sum((H - abs(dh)) * (W - abs(dw)) for dh, dw in SHIFTS)
+FLOPS = 2 * NP * CO * C * B * H * W + 2 * C * CO * B * USED
+
+P = 128
+PACK = 4
+PAIR = 2
+HALVES = 2
+HALF_B = B // HALVES
+STRIP = H * HALF_B
+MAIN_COLS = (W - 1) * STRIP
+EDGE_COLS = H * B
+X_HALF = W * STRIP
+X_MAIN = 2 * EDGE_COLS
+X_COLS = X_MAIN + HALVES * X_HALF
+RUN = 4
+
+PREP_AHEAD = 2
+PACK_LAG = 1
+FUSE_LAG = 2
+
+
+def column_tiles():
+    main = [
+        dict(
+            name="main%d" % g,
+            strips=W - 1,
+            strip_cols=STRIP,
+            row=HALF_B,
+            x_base=X_MAIN + g * X_HALF,
+            x_step=STRIP,
+            pillars=list(range(NP)),
+            half=g,
+        )
+        for g in range(HALVES)
+    ]
+    edge = dict(
+        name="edge",
+        strips=1,
+        strip_cols=EDGE_COLS,
+        row=B,
+        x_base=EDGE_COLS,
+        x_step=EDGE_COLS,
+        pillars=[k for k in range(NP) if SHIFTS[k][1] <= 0],
+        half=None,
+    )
+    return [main[0], edge, main[1]]
+
+
+def valid_part(ct, k):
+    dh, dw = SHIFTS[k]
+    first_strip = 1 if (ct["half"] is not None and dw < 0) else 0
+    return first_strip, max(-dh, 0), H - abs(dh)
+
+
+def tile_shiftedpillarsconcatentation_bnact_np9_pa_kernel(tc, xa, W9, b9, Wf, b_fuse, out):
+    nc = tc.nc
+    tiles = column_tiles()
+    items = [(ct, k) for ct in tiles for k in ct["pillars"]]
+
+    with ExitStack() as stack:
+        keep = stack.enter_context(tc.tile_pool(name="keep", bufs=1))
+        raw_pool = stack.enter_context(tc.tile_pool(name="raw", bufs=4))
+        flow = stack.enter_context(tc.tile_pool(name="flow", bufs=3))
+        work = stack.enter_context(tc.psum_pool(name="work", bufs=4))
+        accs = stack.enter_context(tc.psum_pool(name="accs", bufs=PACK))
+
+        x_raw = []
+        w9_raw = []
+        wf_raw = []
+
+        def load_x(g):
+            xr = keep.tile([P, HALF_B, PACK, H * W], BF16, name="x_raw%d" % g)
+            nc.sync.dma_start(
+                out=xr[:].rearrange("p b t s -> p b (t s)"),
+                in_=xa[g * HALF_B : (g + 1) * HALF_B].rearrange("b (p t) h w -> p b (t h w)", t=PACK),
+            )
+            x_raw.append(xr)
+
+        def load_weights(k):
+            w9r = raw_pool.tile([P, PACK, C], BF16, tag="w9_raw", name="w9_raw%d" % k)
+            nc.sync.dma_start(
+                out=w9r[:].rearrange("p t c -> p (t c)"),
+                in_=W9[k].rearrange("(p t) c -> p (t c)", t=PACK),
+            )
+            w9_raw.append(w9r)
+            wfr = raw_pool.tile([P, PACK, CO], BF16, tag="wf_raw", name="wf_raw%d" % k)
+            nc.sync.dma_start(
+                out=wfr[:],
+                in_=Wf[:, k * CO : (k + 1) * CO].rearrange("(p t) j -> p t j", t=PACK),
+            )
+            wf_raw.append(wfr)
+
+        load_x(0)
+        load_weights(0)
+        load_weights(1)
+        load_x(1)
+        for k in range(2, NP):
+            load_weights(k)
+
+        ident = keep.tile([P, P], F32, name="ident")
+        make_identity(nc, ident[:])
+
+        bias_rows = keep.tile([P, C], BF16, name="bias_rows")
+        nc.vector.memset(bias_rows[:], 0.0)
+        n_rows = NP + 1
+        nc.scalar.dma_start(out=bias_rows[0:NP, :], in_=b9)
+        nc.scalar.dma_start(out=bias_rows[NP:n_rows, :], in_=b_fuse.rearrange("(r c) -> r c", r=1))
+        bias_ps = work.tile([P, PAIR, P], F32, tag="work", name="bias_ps")
+        for u in range(PAIR):
+            nc.tensor.transpose(bias_ps[:, u, :], bias_rows[:].bitcast(F32)[:, u : PAIR * P : PAIR], ident[:])
+        bias_pairs = keep.tile([P, PAIR, n_rows], F32, name="bias_pairs")
+        nc.vector.tensor_copy(out=bias_pairs[:], in_=bias_ps[:, :, 0:n_rows])
+        bias = keep.tile([P, PACK * n_rows], F32, name="bias")
+        nc.vector.tensor_copy(
+            out=bias[:].rearrange("p (r u e) -> p r u e", u=PAIR, e=PAIR),
+            in_=bias_pairs[:].bitcast(BF16).rearrange("p u (r e) -> p r u e", e=PAIR),
+        )
+        fuse_bias = NP * PACK
+
+        stage = {}
+        for ct in tiles:
+            kind = ct["strip_cols"]
+            for k in ct["pillars"]:
+                if (kind, k) in stage:
+                    continue
+                st = keep.tile(
+                    [P, ct["strips"] * ct["strip_cols"], PACK], BF16, name="stage%d_%d" % (kind, k), align_bytes=64
+                )
+                stage[(kind, k)] = st
+                first_strip, first_row, rows = valid_part(ct, k)
+                view = st[:].rearrange("p (w s) t -> p w s t", w=ct["strips"])
+                if first_strip:
+                    nc.vector.memset(view[:, 0:first_strip], 0.0)
+                if rows < H:
+                    empty_row = 0 if first_row else H - 1
+                    nc.vector.memset(view[:, :, empty_row * ct["row"] : (empty_row + 1) * ct["row"], :], 0.0)
+
+        x_grouped = keep.tile([P, X_COLS, PACK], BF16, name="x_grouped", align_bytes=64)
+        x_codes = keep.tile([P, X_COLS], U32, name="x_codes", align_bytes=64)
+        x_scales = keep.tile([P, X_COLS], U8, name="x_scales", align_bytes=64)
+
+        def regroup_x_main(g):
+            lo = X_MAIN + g * X_HALF
+            nc.vector.tensor_copy(
+                out=x_grouped[:, lo : lo + X_HALF, :].rearrange("p (w h b) t -> p w h b t", w=W, h=H),
+                in_=x_raw[g][:].rearrange("p b t (h w) -> p w h b t", w=W),
+            )
+
+        def regroup_x_edge(g):
+            nc.vector.tensor_copy(
+                out=x_grouped[:, 0:X_MAIN, :].rearrange("p (w h g b) t -> p w h g b t", w=2, h=H, g=HALVES)[
+                    :, :, :, g, :, :
+                ],
+                in_=x_raw[g][:].rearrange("p b t (h w) -> p w h b t", w=W)[:, W - 2 : W],
+            )
+
+        def quantise_x(lo, cols):
+            nc.vector.quantize_mx(
+                out=x_codes[:, lo : lo + cols].bitcast(FP8X4),
+                scales=x_scales[:, lo : lo + cols],
+                in_=x_grouped[:, lo : lo + cols, :].rearrange("p c t -> p (c t)"),
+            )
+
+        regroup_x_main(0)
+        regroup_x_edge(0)
+        quantise_x(X_MAIN, 512)
+        regroup_x_edge(1)
+        regroup_x_main(1)
+        quantise_x(0, X_MAIN)
+        quantise_x(X_MAIN + 512, 512)
+        quantise_x(X_MAIN + 1024, 128)
+
+        w9_codes = keep.tile([P, NP, CO], U32, name="w9_codes", align_bytes=64)
+        w9_scales = keep.tile([P, NP, CO], U8, name="w9_scales", align_bytes=64)
+        wf_codes = keep.tile([P, NP, C], U32, name="wf_codes", align_bytes=64)
+        wf_scales = keep.tile([P, NP, C], U8, name="wf_scales", align_bytes=64)
+        banks_emptied = [0]
+
+        def transpose_and_quantise(raw, codes, scales):
+            words = raw[:].bitcast(F32)
+            grouped = flow.tile([P, PACK * P * PACK], BF16, tag="w_grouped", name="w_grouped", bufs=4, align_bytes=64)
+            grouped_words = grouped[:].bitcast(F32)
+            for pair_of_tiles in range(PACK // 2):
+                bank = work.tile([P, PAIR, 2 * P], F32, tag="work", name="w_bank")
+                for i in range(2):
+                    for u in range(PAIR):
+                        nc.tensor.transpose(
+                            bank[:, u, i * P : (i + 1) * P],
+                            words[:, 2 * pair_of_tiles + i, u : PAIR * P : PAIR],
+                            ident[:],
+                        )
+                dst = grouped_words[:, pair_of_tiles * 4 * P : (pair_of_tiles + 1) * 4 * P].rearrange(
+                    "p (c u) -> p c u", u=PAIR
+                )
+                src = bank[:].rearrange("p u c -> p c u")
+                if banks_emptied[0] % 4 == 3:
+                    nc.vector.tensor_copy(out=dst, in_=src)
+                else:
+                    nc.scalar.copy(out=dst, in_=src)
+                banks_emptied[0] += 1
+            nc.vector.quantize_mx(out=codes.bitcast(FP8X4), scales=scales, in_=grouped[:])
+
+        def prepare_weights(k):
+            transpose_and_quantise(w9_raw[k], w9_codes[:, k, :], w9_scales[:, k, :])
+            transpose_and_quantise(wf_raw[k], wf_codes[:, k, :], wf_scales[:, k, :])
+
+        planes_of = {}
+        cat_of = {}
+        acc_of = {}
+        out_sb = [keep.tile([P, B, PAIR, H * W], F32, name="out_sb%d" % u) for u in range(PAIR)]
+        finished = set()
+
+        def project(n):
+            ct, k = items[n]
+            dh, dw = SHIFTS[k]
+            cols = ct["strips"] * ct["strip_cols"]
+            x_lo = ct["x_base"] + dw * ct["x_step"]
+            first_strip, first_row, rows = valid_part(ct, k)
+            dst_lo = first_row * ct["row"]
+            src_lo = (first_row + dh) * ct["row"]
+            span = rows * ct["row"]
+            planes = flow.tile([P, PACK, cols], BF16, tag="planes", name="planes")
+            planes_of[n] = planes
+            for t in range(PACK):
+                y_ps = work.tile([P, cols], F32, tag="work", name="y_ps")
+                nc.tensor.matmul_mx(
+                    out=y_ps[:],
+                    lhsT=w9_codes[:, k, t * P : (t + 1) * P].bitcast(FP8X4),
+                    lhsT_scale=w9_scales[:, k, t * P : (t + 1) * P],
+                    rhs=x_codes[:, x_lo : x_lo + cols].bitcast(FP8X4),
+                    rhs_scale=x_scales[:, x_lo : x_lo + cols],
+                    start=True,
+                    stop=True,
+                )
+                nc.scalar.activation(
+                    out=planes[:, t, :].rearrange("p (w s) -> p w s", w=ct["strips"])[
+                        :, first_strip:, dst_lo : dst_lo + span
+                    ],
+                    in_=y_ps[:].rearrange("p (w s) -> p w s", w=ct["strips"])[:, first_strip:, src_lo : src_lo + span],
+                    func=IDENTITY,
+                    bias=bias[:, k * PACK + t : k * PACK + t + 1],
+                    scale=1.0,
+                )
+
+        def pack(n):
+            ct, k = items[n]
+            cols = ct["strips"] * ct["strip_cols"]
+            first_strip, first_row, rows = valid_part(ct, k)
+            lo = first_row * ct["row"] // RUN
+            hi = lo + rows * ct["row"] // RUN
+            st = stage[(ct["strip_cols"], k)]
+            nc.vector.tensor_copy(
+                out=st[:].rearrange("p (w c i) t -> p w c t i", w=ct["strips"], i=RUN)[:, first_strip:, lo:hi],
+                in_=planes_of[n][:].rearrange("p t (w c i) -> p w c t i", w=ct["strips"], i=RUN)[
+                    :, first_strip:, lo:hi
+                ],
+            )
+            codes = flow.tile([P, cols], U32, tag="cat_codes", name="cat_codes", align_bytes=64)
+            scales = flow.tile([P, cols], U8, tag="cat_scales", name="cat_scales", align_bytes=64)
+            nc.vector.quantize_mx(
+                out=codes[:].bitcast(FP8X4), scales=scales[:], in_=st[:].rearrange("p c t -> p (c t)")
+            )
+            cat_of[n] = (codes, scales)
+
+        def fuse(n):
+            ct, k = items[n]
+            cols = ct["strips"] * ct["strip_cols"]
+            codes, scales = cat_of[n]
+            first = k == ct["pillars"][0]
+            last = k == ct["pillars"][-1]
+            for t in range(PACK):
+                if first:
+                    acc_of[t] = accs.tile([P, cols], F32, tag="acc", name="acc")
+                nc.tensor.matmul_mx(
+                    out=acc_of[t][:],
+                    lhsT=wf_codes[:, k, t * P : (t + 1) * P].bitcast(FP8X4),
+                    lhsT_scale=wf_scales[:, k, t * P : (t + 1) * P],
+                    rhs=codes[:].bitcast(FP8X4),
+                    rhs_scale=scales[:],
+                    start=first,
+                    stop=last,
+                )
+            if last:
+                for t in range(PACK):
+                    empty_accumulator(ct, t)
+                finished.add(ct["name"])
+                for g in range(HALVES):
+                    if ("main%d" % g) in finished and "edge" in finished and ("stored%d" % g) not in finished:
+                        finished.add("stored%d" % g)
+                        store(g)
+
+        def empty_accumulator(ct, t):
+            u, e = divmod(t, PAIR)
+            image = out_sb[u][:, :, e, :].rearrange("p b (h w) -> p b h w", w=W)
+            if ct["half"] is None:
+                dst = image[:, :, :, W - 1]
+                src = acc_of[t][:].rearrange("p (h b) -> p b h", h=H)
+            else:
+                g = ct["half"]
+                dst = image[:, g * HALF_B : (g + 1) * HALF_B, :, 0 : W - 1]
+                src = acc_of[t][:].rearrange("p (w h b) -> p b h w", w=W - 1, h=H)
+            b_col = bias[:, fuse_bias + t : fuse_bias + t + 1]
+            if e == 0:
+                nc.vector.tensor_scalar(out=dst, in0=src, scalar1=b_col, scalar2=None, op0=ADD)
+            else:
+                nc.scalar.activation(out=dst, in_=src, func=IDENTITY, bias=b_col, scale=1.0)
+
+        def store(g):
+            for u in range(PAIR):
+                nc.sync.dma_start(
+                    out=out[g * HALF_B : (g + 1) * HALF_B].rearrange(
+                        "b (p u e) h w -> u p b (e h w)", u=PAIR, e=PAIR
+                    )[u],
+                    in_=out_sb[u][:, g * HALF_B : (g + 1) * HALF_B].rearrange("p b e s -> p b (e s)"),
+                )
+
+        for k in range(PREP_AHEAD):
+            prepare_weights(k)
+        for step in range(len(items) + FUSE_LAG):
+            if step + PREP_AHEAD < NP:
+                prepare_weights(step + PREP_AHEAD)
+            if step < len(items):
+                project(step)
+            if 0 <= step - PACK_LAG < len(items):
+                pack(step - PACK_LAG)
+            if 0 <= step - FUSE_LAG:
+                fuse(step - FUSE_LAG)

@@ -5,6 +5,7 @@ from concourse.masks import make_identity
 
 F32 = mybir.dt.float32
 BF16 = mybir.dt.bfloat16
+I32 = mybir.dt.int32
 U32 = mybir.dt.uint32
 U8 = mybir.dt.uint8
 FP8X4 = mybir.dt.float8_e4m3fn_x4
@@ -24,12 +25,16 @@ HALF_B = B // HALVES
 STRIP = H * HALF_B
 MAIN_COLS = (W - 1) * STRIP
 EDGE_COLS = H * B
+X_PAD = STRIP
 X_HALF = W * STRIP
-X_MAIN = 2 * EDGE_COLS
-X_COLS = X_MAIN + HALVES * X_HALF
+X_EDGE = X_PAD + HALVES * X_HALF
+X_COLS = X_EDGE + 2 * EDGE_COLS
 RUN = 4
 
-PREP_AHEAD = 2
+EDGE_PILLARS = [k for k in range(NP) if SHIFTS[k][1] <= 0]
+PILLARS = EDGE_PILLARS + [k for k in range(NP) if SHIFTS[k][1] > 0]
+
+PROJECT_LAG = 1
 PACK_LAG = 1
 FUSE_LAG = 2
 
@@ -41,9 +46,9 @@ def column_tiles():
             strips=W - 1,
             strip_cols=STRIP,
             row=HALF_B,
-            x_base=X_MAIN + g * X_HALF,
+            x_base=X_PAD + g * X_HALF,
             x_step=STRIP,
-            pillars=list(range(NP)),
+            pillars=PILLARS,
             half=g,
         )
         for g in range(HALVES)
@@ -53,12 +58,12 @@ def column_tiles():
         strips=1,
         strip_cols=EDGE_COLS,
         row=B,
-        x_base=EDGE_COLS,
+        x_base=X_EDGE + EDGE_COLS,
         x_step=EDGE_COLS,
-        pillars=[k for k in range(NP) if SHIFTS[k][1] <= 0],
+        pillars=EDGE_PILLARS,
         half=None,
     )
-    return [main[0], edge, main[1]]
+    return [edge, main[0], main[1]]
 
 
 def valid_part(ct, k):
@@ -79,9 +84,15 @@ def tile_shiftedpillarsconcatentation_bnact_np9_pa_kernel(tc, xa, W9, b9, Wf, b_
         work = stack.enter_context(tc.psum_pool(name="work", bufs=4))
         accs = stack.enter_context(tc.psum_pool(name="accs", bufs=PACK))
 
-        x_raw = []
-        w9_raw = []
-        wf_raw = []
+        n_rows = NP + 1
+        b9_bf = keep.tile([P, NP, PACK], BF16, name="b9_bf")
+        nc.scalar.dma_start(out=b9_bf[:], in_=b9.rearrange("k (p t) -> p k t", t=PACK))
+        bf_bf = keep.tile([P, PACK], BF16, name="bf_bf")
+        nc.scalar.dma_start(out=bf_bf[:], in_=b_fuse.rearrange("(p t) -> p t", t=PACK))
+
+        x_raw = {}
+        w9_raw = {}
+        wf_raw = {}
 
         def load_x(g):
             xr = keep.tile([P, HALF_B, PACK, H * W], BF16, name="x_raw%d" % g)
@@ -89,48 +100,38 @@ def tile_shiftedpillarsconcatentation_bnact_np9_pa_kernel(tc, xa, W9, b9, Wf, b_
                 out=xr[:].rearrange("p b t s -> p b (t s)"),
                 in_=xa[g * HALF_B : (g + 1) * HALF_B].rearrange("b (p t) h w -> p b (t h w)", t=PACK),
             )
-            x_raw.append(xr)
+            x_raw[g] = xr
 
-        def load_weights(k):
+        def load_w9(k):
             w9r = raw_pool.tile([P, PACK, C], BF16, tag="w9_raw", name="w9_raw%d" % k)
             nc.sync.dma_start(
                 out=w9r[:].rearrange("p t c -> p (t c)"),
                 in_=W9[k].rearrange("(p t) c -> p (t c)", t=PACK),
             )
-            w9_raw.append(w9r)
+            w9_raw[k] = w9r
+
+        def load_wf(k):
             wfr = raw_pool.tile([P, PACK, CO], BF16, tag="wf_raw", name="wf_raw%d" % k)
             nc.sync.dma_start(
                 out=wfr[:],
                 in_=Wf[:, k * CO : (k + 1) * CO].rearrange("(p t) j -> p t j", t=PACK),
             )
-            wf_raw.append(wfr)
+            wf_raw[k] = wfr
 
-        load_x(0)
-        load_weights(0)
-        load_weights(1)
-        load_x(1)
-        for k in range(2, NP):
-            load_weights(k)
+        for i, k in enumerate(PILLARS):
+            load_w9(k)
+            load_wf(k)
+            if i == 0:
+                load_x(0)
+                load_x(1)
 
         ident = keep.tile([P, P], F32, name="ident")
         make_identity(nc, ident[:])
 
-        bias_rows = keep.tile([P, C], BF16, name="bias_rows")
-        nc.vector.memset(bias_rows[:], 0.0)
-        n_rows = NP + 1
-        nc.scalar.dma_start(out=bias_rows[0:NP, :], in_=b9)
-        nc.scalar.dma_start(out=bias_rows[NP:n_rows, :], in_=b_fuse.rearrange("(r c) -> r c", r=1))
-        bias_ps = work.tile([P, PAIR, P], F32, tag="work", name="bias_ps")
-        for u in range(PAIR):
-            nc.tensor.transpose(bias_ps[:, u, :], bias_rows[:].bitcast(F32)[:, u : PAIR * P : PAIR], ident[:])
-        bias_pairs = keep.tile([P, PAIR, n_rows], F32, name="bias_pairs")
-        nc.vector.tensor_copy(out=bias_pairs[:], in_=bias_ps[:, :, 0:n_rows])
         bias = keep.tile([P, PACK * n_rows], F32, name="bias")
-        nc.vector.tensor_copy(
-            out=bias[:].rearrange("p (r u e) -> p r u e", u=PAIR, e=PAIR),
-            in_=bias_pairs[:].bitcast(BF16).rearrange("p u (r e) -> p r u e", e=PAIR),
-        )
         fuse_bias = NP * PACK
+        nc.vector.tensor_copy(out=bias[:, 0:fuse_bias], in_=b9_bf[:].rearrange("p r t -> p (r t)"))
+        nc.vector.tensor_copy(out=bias[:, fuse_bias : fuse_bias + PACK], in_=bf_bf[:])
 
         stage = {}
         for ct in tiles:
@@ -145,25 +146,29 @@ def tile_shiftedpillarsconcatentation_bnact_np9_pa_kernel(tc, xa, W9, b9, Wf, b_
                 first_strip, first_row, rows = valid_part(ct, k)
                 view = st[:].rearrange("p (w s) t -> p w s t", w=ct["strips"])
                 if first_strip:
-                    nc.vector.memset(view[:, 0:first_strip], 0.0)
+                    nc.gpsimd.memset(view[:, 0:first_strip], 0.0)
                 if rows < H:
                     empty_row = 0 if first_row else H - 1
-                    nc.vector.memset(view[:, :, empty_row * ct["row"] : (empty_row + 1) * ct["row"], :], 0.0)
+                    nc.gpsimd.memset(view[:, :, empty_row * ct["row"] : (empty_row + 1) * ct["row"], :], 0.0)
 
         x_grouped = keep.tile([P, X_COLS, PACK], BF16, name="x_grouped", align_bytes=64)
         x_codes = keep.tile([P, X_COLS], U32, name="x_codes", align_bytes=64)
         x_scales = keep.tile([P, X_COLS], U8, name="x_scales", align_bytes=64)
+        nc.vector.memset(x_codes[:, 0:X_PAD].bitcast(I32), 0)
+        nc.vector.memset(x_scales[:, 0:X_PAD].bitcast(I32), 0)
 
-        def regroup_x_main(g):
-            lo = X_MAIN + g * X_HALF
-            nc.vector.tensor_copy(
-                out=x_grouped[:, lo : lo + X_HALF, :].rearrange("p (w h b) t -> p w h b t", w=W, h=H),
-                in_=x_raw[g][:].rearrange("p b t (h w) -> p w h b t", w=W),
+        def regroup_x_main(copy, g, w_lo, w_hi):
+            lo = X_PAD + g * X_HALF
+            copy(
+                out=x_grouped[:, lo + w_lo * STRIP : lo + w_hi * STRIP, :].rearrange(
+                    "p (w h b) t -> p w h b t", w=w_hi - w_lo, h=H
+                ),
+                in_=x_raw[g][:].rearrange("p b t (h w) -> p w h b t", w=W)[:, w_lo:w_hi],
             )
 
-        def regroup_x_edge(g):
-            nc.vector.tensor_copy(
-                out=x_grouped[:, 0:X_MAIN, :].rearrange("p (w h g b) t -> p w h g b t", w=2, h=H, g=HALVES)[
+        def regroup_x_edge(copy, g):
+            copy(
+                out=x_grouped[:, X_EDGE:X_COLS, :].rearrange("p (w h g b) t -> p w h g b t", w=2, h=H, g=HALVES)[
                     :, :, :, g, :, :
                 ],
                 in_=x_raw[g][:].rearrange("p b t (h w) -> p w h b t", w=W)[:, W - 2 : W],
@@ -176,20 +181,28 @@ def tile_shiftedpillarsconcatentation_bnact_np9_pa_kernel(tc, xa, W9, b9, Wf, b_
                 in_=x_grouped[:, lo : lo + cols, :].rearrange("p c t -> p (c t)"),
             )
 
-        regroup_x_main(0)
-        regroup_x_edge(0)
-        quantise_x(X_MAIN, 512)
-        regroup_x_edge(1)
-        regroup_x_main(1)
-        quantise_x(0, X_MAIN)
-        quantise_x(X_MAIN + 512, 512)
-        quantise_x(X_MAIN + 1024, 128)
+        on_vector = nc.vector.tensor_copy
+        on_scalar = nc.scalar.copy
+        x_jobs = {
+            0: [
+                lambda: regroup_x_edge(on_vector, 0),
+                lambda: regroup_x_edge(on_vector, 1),
+                lambda: quantise_x(X_EDGE, 2 * EDGE_COLS),
+            ],
+            2: [lambda: regroup_x_main(on_vector, 0, 0, 3)],
+            3: [lambda: regroup_x_main(on_scalar, 0, 3, 6)],
+            4: [lambda: regroup_x_main(on_vector, 0, 6, W)],
+            5: [lambda: quantise_x(X_PAD, MAIN_COLS), lambda: quantise_x(X_PAD + MAIN_COLS, STRIP)],
+            6: [lambda: regroup_x_main(on_vector, 1, 0, 3)],
+            7: [lambda: regroup_x_main(on_scalar, 1, 3, 6)],
+            8: [lambda: regroup_x_main(on_vector, 1, 6, W)],
+            9: [lambda: quantise_x(X_PAD + X_HALF, MAIN_COLS), lambda: quantise_x(X_PAD + X_HALF + MAIN_COLS, STRIP)],
+        }
 
         w9_codes = keep.tile([P, NP, CO], U32, name="w9_codes", align_bytes=64)
         w9_scales = keep.tile([P, NP, CO], U8, name="w9_scales", align_bytes=64)
         wf_codes = keep.tile([P, NP, C], U32, name="wf_codes", align_bytes=64)
         wf_scales = keep.tile([P, NP, C], U8, name="wf_scales", align_bytes=64)
-        banks_emptied = [0]
 
         def transpose_and_quantise(raw, codes, scales):
             words = raw[:].bitcast(F32)
@@ -208,15 +221,13 @@ def tile_shiftedpillarsconcatentation_bnact_np9_pa_kernel(tc, xa, W9, b9, Wf, b_
                     "p (c u) -> p c u", u=PAIR
                 )
                 src = bank[:].rearrange("p u c -> p c u")
-                if banks_emptied[0] % 4 == 3:
-                    nc.vector.tensor_copy(out=dst, in_=src)
-                else:
-                    nc.scalar.copy(out=dst, in_=src)
-                banks_emptied[0] += 1
+                nc.scalar.copy(out=dst, in_=src)
             nc.vector.quantize_mx(out=codes.bitcast(FP8X4), scales=scales, in_=grouped[:])
 
-        def prepare_weights(k):
+        def prepare_w9(k):
             transpose_and_quantise(w9_raw[k], w9_codes[:, k, :], w9_scales[:, k, :])
+
+        def prepare_wf(k):
             transpose_and_quantise(wf_raw[k], wf_codes[:, k, :], wf_scales[:, k, :])
 
         planes_of = {}
@@ -234,6 +245,25 @@ def tile_shiftedpillarsconcatentation_bnact_np9_pa_kernel(tc, xa, W9, b9, Wf, b_
             dst_lo = first_row * ct["row"]
             src_lo = (first_row + dh) * ct["row"]
             span = rows * ct["row"]
+            if ct["half"] is None:
+                y_bank = work.tile([P, PACK, cols], F32, tag="work", name="y_bank")
+                for t in range(PACK):
+                    nc.tensor.matmul_mx(
+                        out=y_bank[:, t, :],
+                        lhsT=w9_codes[:, k, t * P : (t + 1) * P].bitcast(FP8X4),
+                        lhsT_scale=w9_scales[:, k, t * P : (t + 1) * P],
+                        rhs=x_codes[:, x_lo : x_lo + cols].bitcast(FP8X4),
+                        rhs_scale=x_scales[:, x_lo : x_lo + cols],
+                        start=True,
+                        stop=True,
+                    )
+                nc.vector.tensor_tensor(
+                    out=stage[(ct["strip_cols"], k)][:, dst_lo : dst_lo + span, :],
+                    in0=y_bank[:].rearrange("p t c -> p c t")[:, src_lo : src_lo + span, :],
+                    in1=bias[:, k * PACK : (k + 1) * PACK].unsqueeze(1).to_broadcast([P, span, PACK]),
+                    op=ADD,
+                )
+                return
             planes = flow.tile([P, PACK, cols], BF16, tag="planes", name="planes")
             planes_of[n] = planes
             for t in range(PACK):
@@ -264,12 +294,13 @@ def tile_shiftedpillarsconcatentation_bnact_np9_pa_kernel(tc, xa, W9, b9, Wf, b_
             lo = first_row * ct["row"] // RUN
             hi = lo + rows * ct["row"] // RUN
             st = stage[(ct["strip_cols"], k)]
-            nc.vector.tensor_copy(
-                out=st[:].rearrange("p (w c i) t -> p w c t i", w=ct["strips"], i=RUN)[:, first_strip:, lo:hi],
-                in_=planes_of[n][:].rearrange("p t (w c i) -> p w c t i", w=ct["strips"], i=RUN)[
-                    :, first_strip:, lo:hi
-                ],
-            )
+            if ct["half"] is not None:
+                nc.vector.tensor_copy(
+                    out=st[:].rearrange("p (w c i) t -> p w c t i", w=ct["strips"], i=RUN)[:, first_strip:, lo:hi],
+                    in_=planes_of[n][:].rearrange("p t (w c i) -> p w c t i", w=ct["strips"], i=RUN)[
+                        :, first_strip:, lo:hi
+                    ],
+                )
             codes = flow.tile([P, cols], U32, tag="cat_codes", name="cat_codes", align_bytes=64)
             scales = flow.tile([P, cols], U8, tag="cat_scales", name="cat_scales", align_bytes=64)
             nc.vector.quantize_mx(
@@ -329,14 +360,16 @@ def tile_shiftedpillarsconcatentation_bnact_np9_pa_kernel(tc, xa, W9, b9, Wf, b_
                     in_=out_sb[u][:, g * HALF_B : (g + 1) * HALF_B].rearrange("p b e s -> p b (e s)"),
                 )
 
-        for k in range(PREP_AHEAD):
-            prepare_weights(k)
-        for step in range(len(items) + FUSE_LAG):
-            if step + PREP_AHEAD < NP:
-                prepare_weights(step + PREP_AHEAD)
-            if step < len(items):
-                project(step)
-            if 0 <= step - PACK_LAG < len(items):
-                pack(step - PACK_LAG)
-            if 0 <= step - FUSE_LAG:
-                fuse(step - FUSE_LAG)
+        for step in range(len(items) + PROJECT_LAG + FUSE_LAG):
+            if step < NP:
+                prepare_w9(PILLARS[step])
+                prepare_wf(PILLARS[step])
+            for job in x_jobs.get(step, []):
+                job()
+            n = step - PROJECT_LAG
+            if 0 <= n < len(items):
+                project(n)
+            if 0 <= n - PACK_LAG < len(items):
+                pack(n - PACK_LAG)
+            if 0 <= n - FUSE_LAG < len(items):
+                fuse(n - FUSE_LAG)

@@ -33,49 +33,22 @@ RUN = 4
 
 EDGE_PILLARS = [k for k in range(NP) if SHIFTS[k][1] <= 0]
 PILLARS = EDGE_PILLARS + [k for k in range(NP) if SHIFTS[k][1] > 0]
+N_EDGE = len(EDGE_PILLARS)
+N_MAIN = HALVES * NP
 
-PROJECT_LAG = 1
-PACK_LAG = 1
+EDGE_LAG = 3
 FUSE_LAG = 2
+EDGE_FUSE_SLOT = NP + 1
 
 
-def column_tiles():
-    main = [
-        dict(
-            name="main%d" % g,
-            strips=W - 1,
-            strip_cols=STRIP,
-            row=HALF_B,
-            x_base=X_PAD + g * X_HALF,
-            x_step=STRIP,
-            pillars=PILLARS,
-            half=g,
-        )
-        for g in range(HALVES)
-    ]
-    edge = dict(
-        name="edge",
-        strips=1,
-        strip_cols=EDGE_COLS,
-        row=B,
-        x_base=X_EDGE + EDGE_COLS,
-        x_step=EDGE_COLS,
-        pillars=EDGE_PILLARS,
-        half=None,
-    )
-    return [edge, main[0], main[1]]
-
-
-def valid_part(ct, k):
+def valid_part(main, k):
     dh, dw = SHIFTS[k]
-    first_strip = 1 if (ct["half"] is not None and dw < 0) else 0
+    first_strip = 1 if (main and dw < 0) else 0
     return first_strip, max(-dh, 0), H - abs(dh)
 
 
 def tile_shiftedpillarsconcatentation_bnact_np9_pa_kernel(tc, xa, W9, b9, Wf, b_fuse, out):
     nc = tc.nc
-    tiles = column_tiles()
-    items = [(ct, k) for ct in tiles for k in ct["pillars"]]
 
     with ExitStack() as stack:
         keep = stack.enter_context(tc.tile_pool(name="keep", bufs=1))
@@ -83,16 +56,15 @@ def tile_shiftedpillarsconcatentation_bnact_np9_pa_kernel(tc, xa, W9, b9, Wf, b_
         flow = stack.enter_context(tc.tile_pool(name="flow", bufs=3))
         work = stack.enter_context(tc.psum_pool(name="work", bufs=4))
         accs = stack.enter_context(tc.psum_pool(name="accs", bufs=PACK))
+        stack.enter_context(tc.manual_schedule())
 
-        n_rows = NP + 1
         b9_bf = keep.tile([P, NP, PACK], BF16, name="b9_bf")
         nc.scalar.dma_start(out=b9_bf[:], in_=b9.rearrange("k (p t) -> p k t", t=PACK))
         bf_bf = keep.tile([P, PACK], BF16, name="bf_bf")
         nc.scalar.dma_start(out=bf_bf[:], in_=b_fuse.rearrange("(p t) -> p t", t=PACK))
 
         x_raw = {}
-        w9_raw = {}
-        wf_raw = {}
+        raw_of = {}
 
         def load_x(g):
             xr = keep.tile([P, HALF_B, PACK, H * W], BF16, name="x_raw%d" % g)
@@ -102,54 +74,55 @@ def tile_shiftedpillarsconcatentation_bnact_np9_pa_kernel(tc, xa, W9, b9, Wf, b_
             )
             x_raw[g] = xr
 
-        def load_w9(k):
+        def load_w9(i):
+            k = PILLARS[i]
             w9r = raw_pool.tile([P, PACK, C], BF16, tag="w9_raw", name="w9_raw%d" % k)
             nc.sync.dma_start(
                 out=w9r[:].rearrange("p t c -> p (t c)"),
                 in_=W9[k].rearrange("(p t) c -> p (t c)", t=PACK),
             )
-            w9_raw[k] = w9r
+            raw_of[("w9", i)] = w9r
 
-        def load_wf(k):
+        def load_wf(i):
+            k = PILLARS[i]
             wfr = raw_pool.tile([P, PACK, CO], BF16, tag="wf_raw", name="wf_raw%d" % k)
             nc.sync.dma_start(
                 out=wfr[:],
                 in_=Wf[:, k * CO : (k + 1) * CO].rearrange("(p t) j -> p t j", t=PACK),
             )
-            wf_raw[k] = wfr
+            raw_of[("wf", i)] = wfr
 
-        for i, k in enumerate(PILLARS):
-            load_w9(k)
-            load_wf(k)
+        for i in range(NP):
+            load_w9(i)
             if i == 0:
                 load_x(0)
+            load_wf(i)
+            if i == 2:
                 load_x(1)
 
         ident = keep.tile([P, P], F32, name="ident")
         make_identity(nc, ident[:])
 
-        bias = keep.tile([P, PACK * n_rows], F32, name="bias")
+        bias = keep.tile([P, PACK * (NP + 1)], F32, name="bias")
         fuse_bias = NP * PACK
         nc.vector.tensor_copy(out=bias[:, 0:fuse_bias], in_=b9_bf[:].rearrange("p r t -> p (r t)"))
         nc.vector.tensor_copy(out=bias[:, fuse_bias : fuse_bias + PACK], in_=bf_bf[:])
 
         stage = {}
-        for ct in tiles:
-            kind = ct["strip_cols"]
-            for k in ct["pillars"]:
-                if (kind, k) in stage:
-                    continue
+        for main in (True, False):
+            strips, strip_cols, row = (W - 1, STRIP, HALF_B) if main else (1, EDGE_COLS, B)
+            for k in PILLARS if main else EDGE_PILLARS:
                 st = keep.tile(
-                    [P, ct["strips"] * ct["strip_cols"], PACK], BF16, name="stage%d_%d" % (kind, k), align_bytes=64
+                    [P, strips * strip_cols, PACK], BF16, name="stage%d_%d" % (strip_cols, k), align_bytes=64
                 )
-                stage[(kind, k)] = st
-                first_strip, first_row, rows = valid_part(ct, k)
-                view = st[:].rearrange("p (w s) t -> p w s t", w=ct["strips"])
+                stage[(main, k)] = st
+                first_strip, first_row, rows = valid_part(main, k)
+                view = st[:].rearrange("p (w s) t -> p w s t", w=strips)
                 if first_strip:
                     nc.gpsimd.memset(view[:, 0:first_strip], 0.0)
                 if rows < H:
                     empty_row = 0 if first_row else H - 1
-                    nc.gpsimd.memset(view[:, :, empty_row * ct["row"] : (empty_row + 1) * ct["row"], :], 0.0)
+                    nc.gpsimd.memset(view[:, :, empty_row * row : (empty_row + 1) * row, :], 0.0)
 
         x_grouped = keep.tile([P, X_COLS, PACK], BF16, name="x_grouped", align_bytes=64)
         x_codes = keep.tile([P, X_COLS], U32, name="x_codes", align_bytes=64)
@@ -184,172 +157,143 @@ def tile_shiftedpillarsconcatentation_bnact_np9_pa_kernel(tc, xa, W9, b9, Wf, b_
         on_vector = nc.vector.tensor_copy
         on_scalar = nc.scalar.copy
         x_jobs = {
-            0: [
-                lambda: regroup_x_edge(on_vector, 0),
-                lambda: regroup_x_edge(on_vector, 1),
-                lambda: quantise_x(X_EDGE, 2 * EDGE_COLS),
-            ],
-            2: [lambda: regroup_x_main(on_vector, 0, 0, 3)],
-            3: [lambda: regroup_x_main(on_scalar, 0, 3, 6)],
-            4: [lambda: regroup_x_main(on_vector, 0, 6, W)],
-            5: [lambda: quantise_x(X_PAD, MAIN_COLS), lambda: quantise_x(X_PAD + MAIN_COLS, STRIP)],
-            6: [lambda: regroup_x_main(on_vector, 1, 0, 3)],
-            7: [lambda: regroup_x_main(on_scalar, 1, 3, 6)],
-            8: [lambda: regroup_x_main(on_vector, 1, 6, W)],
-            9: [lambda: quantise_x(X_PAD + X_HALF, MAIN_COLS), lambda: quantise_x(X_PAD + X_HALF + MAIN_COLS, STRIP)],
+            0: [lambda: regroup_x_main(on_vector, 0, W - 1, W)],
+            1: [lambda: quantise_x(X_PAD + MAIN_COLS, STRIP), lambda: regroup_x_edge(on_vector, 0)],
+            2: [lambda: regroup_x_edge(on_vector, 1), lambda: quantise_x(X_EDGE, 2 * EDGE_COLS)],
+            3: [lambda: regroup_x_main(on_vector, 1, 0, 3)],
+            4: [lambda: regroup_x_main(on_vector, 1, 3, 6)],
+            5: [lambda: regroup_x_main(on_vector, 1, 6, W)],
+            6: [lambda: quantise_x(X_PAD + X_HALF, MAIN_COLS), lambda: quantise_x(X_PAD + X_HALF + MAIN_COLS, STRIP)],
         }
 
-        w9_codes = keep.tile([P, NP, CO], U32, name="w9_codes", align_bytes=64)
-        w9_scales = keep.tile([P, NP, CO], U8, name="w9_scales", align_bytes=64)
-        wf_codes = keep.tile([P, NP, C], U32, name="wf_codes", align_bytes=64)
-        wf_scales = keep.tile([P, NP, C], U8, name="wf_scales", align_bytes=64)
+        codes_of = {
+            "w9": keep.tile([P, NP, CO], U32, name="w9_codes", align_bytes=64),
+            "wf": keep.tile([P, NP, C], U32, name="wf_codes", align_bytes=64),
+        }
+        scales_of = {
+            "w9": keep.tile([P, NP, CO], U8, name="w9_scales", align_bytes=64),
+            "wf": keep.tile([P, NP, C], U8, name="wf_scales", align_bytes=64),
+        }
+        grouped_of = {}
 
-        def transpose_and_quantise(raw, codes, scales):
-            words = raw[:].bitcast(F32)
+        def transpose_weight(kind, i):
+            words = raw_of[(kind, i)][:].bitcast(F32)
             grouped = flow.tile([P, PACK * P * PACK], BF16, tag="w_grouped", name="w_grouped", bufs=4, align_bytes=64)
+            grouped_of[(kind, i)] = grouped
             grouped_words = grouped[:].bitcast(F32)
             for pair_of_tiles in range(PACK // 2):
                 bank = work.tile([P, PAIR, 2 * P], F32, tag="work", name="w_bank")
-                for i in range(2):
+                for r in range(2):
                     for u in range(PAIR):
                         nc.tensor.transpose(
-                            bank[:, u, i * P : (i + 1) * P],
-                            words[:, 2 * pair_of_tiles + i, u : PAIR * P : PAIR],
+                            bank[:, u, r * P : (r + 1) * P],
+                            words[:, 2 * pair_of_tiles + r, u : PAIR * P : PAIR],
                             ident[:],
                         )
-                dst = grouped_words[:, pair_of_tiles * 4 * P : (pair_of_tiles + 1) * 4 * P].rearrange(
-                    "p (c u) -> p c u", u=PAIR
+                nc.scalar.copy(
+                    out=grouped_words[:, pair_of_tiles * 4 * P : (pair_of_tiles + 1) * 4 * P].rearrange(
+                        "p (c u) -> p c u", u=PAIR
+                    ),
+                    in_=bank[:].rearrange("p u c -> p c u"),
                 )
-                src = bank[:].rearrange("p u c -> p c u")
-                nc.scalar.copy(out=dst, in_=src)
-            nc.vector.quantize_mx(out=codes.bitcast(FP8X4), scales=scales, in_=grouped[:])
 
-        def prepare_w9(k):
-            transpose_and_quantise(w9_raw[k], w9_codes[:, k, :], w9_scales[:, k, :])
+        def quantise_weight(kind, i):
+            nc.vector.quantize_mx(
+                out=codes_of[kind][:, i, :].bitcast(FP8X4), scales=scales_of[kind][:, i, :], in_=grouped_of[(kind, i)][:]
+            )
 
-        def prepare_wf(k):
-            transpose_and_quantise(wf_raw[k], wf_codes[:, k, :], wf_scales[:, k, :])
+        def weight_tile(kind, i, t):
+            return dict(
+                lhsT=codes_of[kind][:, i, t * P : (t + 1) * P].bitcast(FP8X4),
+                lhsT_scale=scales_of[kind][:, i, t * P : (t + 1) * P],
+            )
 
         planes_of = {}
         cat_of = {}
         acc_of = {}
         out_sb = [keep.tile([P, B, PAIR, H * W], F32, name="out_sb%d" % u) for u in range(PAIR)]
-        finished = set()
 
         def project(n):
-            ct, k = items[n]
+            g, i = divmod(n, NP)
+            k = PILLARS[i]
             dh, dw = SHIFTS[k]
-            cols = ct["strips"] * ct["strip_cols"]
-            x_lo = ct["x_base"] + dw * ct["x_step"]
-            first_strip, first_row, rows = valid_part(ct, k)
-            dst_lo = first_row * ct["row"]
-            src_lo = (first_row + dh) * ct["row"]
-            span = rows * ct["row"]
-            if ct["half"] is None:
-                y_bank = work.tile([P, PACK, cols], F32, tag="work", name="y_bank")
-                for t in range(PACK):
-                    nc.tensor.matmul_mx(
-                        out=y_bank[:, t, :],
-                        lhsT=w9_codes[:, k, t * P : (t + 1) * P].bitcast(FP8X4),
-                        lhsT_scale=w9_scales[:, k, t * P : (t + 1) * P],
-                        rhs=x_codes[:, x_lo : x_lo + cols].bitcast(FP8X4),
-                        rhs_scale=x_scales[:, x_lo : x_lo + cols],
-                        start=True,
-                        stop=True,
-                    )
-                nc.vector.tensor_tensor(
-                    out=stage[(ct["strip_cols"], k)][:, dst_lo : dst_lo + span, :],
-                    in0=y_bank[:].rearrange("p t c -> p c t")[:, src_lo : src_lo + span, :],
-                    in1=bias[:, k * PACK : (k + 1) * PACK].unsqueeze(1).to_broadcast([P, span, PACK]),
-                    op=ADD,
-                )
-                return
-            planes = flow.tile([P, PACK, cols], BF16, tag="planes", name="planes")
+            x_lo = X_PAD + g * X_HALF + dw * STRIP
+            first_strip, first_row, rows = valid_part(True, k)
+            dst_lo = first_row * HALF_B
+            src_lo = (first_row + dh) * HALF_B
+            span = rows * HALF_B
+            planes = flow.tile([P, PACK, MAIN_COLS], BF16, tag="planes", name="planes")
             planes_of[n] = planes
             for t in range(PACK):
-                y_ps = work.tile([P, cols], F32, tag="work", name="y_ps")
+                y_ps = work.tile([P, MAIN_COLS], F32, tag="work", name="y_ps")
                 nc.tensor.matmul_mx(
                     out=y_ps[:],
-                    lhsT=w9_codes[:, k, t * P : (t + 1) * P].bitcast(FP8X4),
-                    lhsT_scale=w9_scales[:, k, t * P : (t + 1) * P],
-                    rhs=x_codes[:, x_lo : x_lo + cols].bitcast(FP8X4),
-                    rhs_scale=x_scales[:, x_lo : x_lo + cols],
+                    rhs=x_codes[:, x_lo : x_lo + MAIN_COLS].bitcast(FP8X4),
+                    rhs_scale=x_scales[:, x_lo : x_lo + MAIN_COLS],
                     start=True,
                     stop=True,
+                    **weight_tile("w9", i, t)
                 )
                 nc.scalar.activation(
-                    out=planes[:, t, :].rearrange("p (w s) -> p w s", w=ct["strips"])[
-                        :, first_strip:, dst_lo : dst_lo + span
-                    ],
-                    in_=y_ps[:].rearrange("p (w s) -> p w s", w=ct["strips"])[:, first_strip:, src_lo : src_lo + span],
+                    out=planes[:, t, :].rearrange("p (w s) -> p w s", w=W - 1)[:, first_strip:, dst_lo : dst_lo + span],
+                    in_=y_ps[:].rearrange("p (w s) -> p w s", w=W - 1)[:, first_strip:, src_lo : src_lo + span],
                     func=IDENTITY,
                     bias=bias[:, k * PACK + t : k * PACK + t + 1],
                     scale=1.0,
                 )
 
-        def pack(n):
-            ct, k = items[n]
-            cols = ct["strips"] * ct["strip_cols"]
-            first_strip, first_row, rows = valid_part(ct, k)
-            lo = first_row * ct["row"] // RUN
-            hi = lo + rows * ct["row"] // RUN
-            st = stage[(ct["strip_cols"], k)]
-            if ct["half"] is not None:
-                nc.vector.tensor_copy(
-                    out=st[:].rearrange("p (w c i) t -> p w c t i", w=ct["strips"], i=RUN)[:, first_strip:, lo:hi],
-                    in_=planes_of[n][:].rearrange("p t (w c i) -> p w c t i", w=ct["strips"], i=RUN)[
-                        :, first_strip:, lo:hi
-                    ],
-                )
-            codes = flow.tile([P, cols], U32, tag="cat_codes", name="cat_codes", align_bytes=64)
-            scales = flow.tile([P, cols], U8, tag="cat_scales", name="cat_scales", align_bytes=64)
+        def interleave(n):
+            k = PILLARS[n % NP]
+            first_strip, first_row, rows = valid_part(True, k)
+            lo = first_row * HALF_B // RUN
+            hi = lo + rows * HALF_B // RUN
+            nc.vector.tensor_copy(
+                out=stage[(True, k)][:].rearrange("p (w c r) t -> p w c t r", w=W - 1, r=RUN)[:, first_strip:, lo:hi],
+                in_=planes_of[n][:].rearrange("p t (w c r) -> p w c t r", w=W - 1, r=RUN)[:, first_strip:, lo:hi],
+            )
+
+        def quantise_cat(n):
+            k = PILLARS[n % NP]
+            codes = flow.tile([P, MAIN_COLS], U32, tag="cat_codes", name="cat_codes", align_bytes=64)
+            scales = flow.tile([P, MAIN_COLS], U8, tag="cat_scales", name="cat_scales", align_bytes=64)
             nc.vector.quantize_mx(
-                out=codes[:].bitcast(FP8X4), scales=scales[:], in_=st[:].rearrange("p c t -> p (c t)")
+                out=codes[:].bitcast(FP8X4), scales=scales[:], in_=stage[(True, k)][:].rearrange("p c t -> p (c t)")
             )
             cat_of[n] = (codes, scales)
 
         def fuse(n):
-            ct, k = items[n]
-            cols = ct["strips"] * ct["strip_cols"]
+            i = n % NP
             codes, scales = cat_of[n]
-            first = k == ct["pillars"][0]
-            last = k == ct["pillars"][-1]
             for t in range(PACK):
-                if first:
-                    acc_of[t] = accs.tile([P, cols], F32, tag="acc", name="acc")
+                if i == 0:
+                    acc_of[t] = accs.tile([P, MAIN_COLS], F32, tag="acc", name="acc")
                 nc.tensor.matmul_mx(
                     out=acc_of[t][:],
-                    lhsT=wf_codes[:, k, t * P : (t + 1) * P].bitcast(FP8X4),
-                    lhsT_scale=wf_scales[:, k, t * P : (t + 1) * P],
                     rhs=codes[:].bitcast(FP8X4),
                     rhs_scale=scales[:],
-                    start=first,
-                    stop=last,
+                    start=i == 0,
+                    stop=i == NP - 1,
+                    **weight_tile("wf", i, t)
                 )
-            if last:
-                for t in range(PACK):
-                    empty_accumulator(ct, t)
-                finished.add(ct["name"])
-                for g in range(HALVES):
-                    if ("main%d" % g) in finished and "edge" in finished and ("stored%d" % g) not in finished:
-                        finished.add("stored%d" % g)
-                        store(g)
 
-        def empty_accumulator(ct, t):
-            u, e = divmod(t, PAIR)
-            image = out_sb[u][:, :, e, :].rearrange("p b (h w) -> p b h w", w=W)
-            if ct["half"] is None:
-                dst = image[:, :, :, W - 1]
-                src = acc_of[t][:].rearrange("p (h b) -> p b h", h=H)
-            else:
-                g = ct["half"]
-                dst = image[:, g * HALF_B : (g + 1) * HALF_B, :, 0 : W - 1]
-                src = acc_of[t][:].rearrange("p (w h b) -> p b h w", w=W - 1, h=H)
+        def add_fuse_bias(t, dst, src):
             b_col = bias[:, fuse_bias + t : fuse_bias + t + 1]
-            if e == 0:
+            if t % PAIR == 0:
                 nc.vector.tensor_scalar(out=dst, in0=src, scalar1=b_col, scalar2=None, op0=ADD)
             else:
                 nc.scalar.activation(out=dst, in_=src, func=IDENTITY, bias=b_col, scale=1.0)
+
+        def image_of(t):
+            u, e = divmod(t, PAIR)
+            return out_sb[u][:, :, e, :].rearrange("p b (h w) -> p b h w", w=W)
+
+        def empty_main(g):
+            for t in range(PACK):
+                add_fuse_bias(
+                    t,
+                    image_of(t)[:, g * HALF_B : (g + 1) * HALF_B, :, 0 : W - 1],
+                    acc_of[t][:].rearrange("p (w h b) -> p b h w", w=W - 1, h=H),
+                )
 
         def store(g):
             for u in range(PAIR):
@@ -360,16 +304,101 @@ def tile_shiftedpillarsconcatentation_bnact_np9_pa_kernel(tc, xa, W9, b9, Wf, b_
                     in_=out_sb[u][:, g * HALF_B : (g + 1) * HALF_B].rearrange("p b e s -> p b (e s)"),
                 )
 
-        for step in range(len(items) + PROJECT_LAG + FUSE_LAG):
-            if step < NP:
-                prepare_w9(PILLARS[step])
-                prepare_wf(PILLARS[step])
-            for job in x_jobs.get(step, []):
+        edge_codes = keep.tile([P, N_EDGE, EDGE_COLS], U32, name="edge_codes", align_bytes=64)
+        edge_scales = keep.tile([P, N_EDGE, EDGE_COLS], U8, name="edge_scales", align_bytes=64)
+        edge_bank = {}
+
+        def edge_project(j):
+            x_lo = X_EDGE + EDGE_COLS + SHIFTS[PILLARS[j]][1] * EDGE_COLS
+            y_bank = work.tile([P, PACK, EDGE_COLS], F32, tag="work", name="y_bank")
+            edge_bank[j] = y_bank
+            for t in range(PACK):
+                nc.tensor.matmul_mx(
+                    out=y_bank[:, t, :],
+                    rhs=x_codes[:, x_lo : x_lo + EDGE_COLS].bitcast(FP8X4),
+                    rhs_scale=x_scales[:, x_lo : x_lo + EDGE_COLS],
+                    start=True,
+                    stop=True,
+                    **weight_tile("w9", j, t)
+                )
+
+        def edge_interleave(j):
+            k = PILLARS[j]
+            first_strip, first_row, rows = valid_part(False, k)
+            dst_lo = first_row * B
+            src_lo = (first_row + SHIFTS[k][0]) * B
+            span = rows * B
+            nc.vector.tensor_tensor(
+                out=stage[(False, k)][:, dst_lo : dst_lo + span, :],
+                in0=edge_bank[j][:].rearrange("p t c -> p c t")[:, src_lo : src_lo + span, :],
+                in1=bias[:, k * PACK : (k + 1) * PACK].unsqueeze(1).to_broadcast([P, span, PACK]),
+                op=ADD,
+            )
+
+        def edge_quantise(j):
+            nc.vector.quantize_mx(
+                out=edge_codes[:, j, :].bitcast(FP8X4),
+                scales=edge_scales[:, j, :],
+                in_=stage[(False, PILLARS[j])][:].rearrange("p c t -> p (c t)"),
+            )
+
+        def edge_fuse():
+            bank = work.tile([P, PACK, EDGE_COLS], F32, tag="work", name="edge_acc")
+            for t in range(PACK):
+                for j in range(N_EDGE):
+                    nc.tensor.matmul_mx(
+                        out=bank[:, t, :],
+                        rhs=edge_codes[:, j, :].bitcast(FP8X4),
+                        rhs_scale=edge_scales[:, j, :],
+                        start=j == 0,
+                        stop=j == N_EDGE - 1,
+                        **weight_tile("wf", j, t)
+                    )
+            return bank
+
+        def empty_edge(bank):
+            for t in range(PACK):
+                add_fuse_bias(t, image_of(t)[:, :, :, W - 1], bank[:, t, :].rearrange("p (h b) -> p b h", h=H))
+
+        for s in range(-1, N_MAIN + FUSE_LAG):
+            j = s - EDGE_LAG
+            if 0 <= s < NP:
+                transpose_weight("wf", s)
+            if 0 <= s + 1 < NP:
+                transpose_weight("w9", s + 1)
+            if s == -1:
+                regroup_x_main(on_vector, 0, 0, 5)
+                regroup_x_main(on_scalar, 0, 5, W - 1)
+            if 0 <= j < N_EDGE:
+                edge_project(j)
+            if 0 <= s < N_MAIN:
+                project(s)
+            if 0 <= s - FUSE_LAG < N_MAIN:
+                fuse(s - FUSE_LAG)
+            edge_acc = edge_fuse() if s == EDGE_FUSE_SLOT else None
+
+            if 0 <= s - 1 < N_MAIN:
+                interleave(s - 1)
+            if 0 <= s < NP:
+                quantise_weight("wf", s)
+            if 0 <= j < N_EDGE:
+                edge_interleave(j)
+            if 0 <= s - 1 < N_MAIN:
+                quantise_cat(s - 1)
+            if 0 <= s + 1 < NP:
+                quantise_weight("w9", s + 1)
+            if s == -1:
+                quantise_x(X_PAD, MAIN_COLS)
+            if 0 <= j - 1 < N_EDGE:
+                edge_quantise(j - 1)
+            for job in x_jobs.get(s, []):
                 job()
-            n = step - PROJECT_LAG
-            if 0 <= n < len(items):
-                project(n)
-            if 0 <= n - PACK_LAG < len(items):
-                pack(n - PACK_LAG)
-            if 0 <= n - FUSE_LAG < len(items):
-                fuse(n - FUSE_LAG)
+
+            if s - FUSE_LAG == NP - 1:
+                empty_main(0)
+            if s == EDGE_FUSE_SLOT:
+                empty_edge(edge_acc)
+                store(0)
+            if s - FUSE_LAG == N_MAIN - 1:
+                empty_main(1)
+                store(1)

@@ -356,9 +356,20 @@ def tile_shiftedpillarsconcatentation_bnact_np9_pa_kernel(tc, xa, W9, b9, Wf, b_
                     )
             return bank
 
+        edge_out = keep.tile([P, PACK, EDGE_COLS], F32, name="edge_out")
+
         def empty_edge(bank):
+            nc.vector.tensor_tensor(
+                out=edge_out[:],
+                in0=bank[:],
+                in1=bias[:, fuse_bias : fuse_bias + PACK].unsqueeze(2).to_broadcast([P, PACK, EDGE_COLS]),
+                op=ADD,
+            )
+
+        def scatter_edge():
             for t in range(PACK):
-                add_fuse_bias(t, image_of(t)[:, :, :, W - 1], bank[:, t, :].rearrange("p (h b) -> p b h", h=H))
+                copy = on_vector if t % PAIR == 0 else on_scalar
+                copy(out=image_of(t)[:, :, :, W - 1], in_=edge_out[:, t, :].rearrange("p (h b) -> p b h", h=H))
 
         for s in range(-1, N_MAIN + FUSE_LAG):
             j = s - EDGE_LAG
@@ -375,7 +386,8 @@ def tile_shiftedpillarsconcatentation_bnact_np9_pa_kernel(tc, xa, W9, b9, Wf, b_
                 project(s)
             if 0 <= s - FUSE_LAG < N_MAIN:
                 fuse(s - FUSE_LAG)
-            edge_acc = edge_fuse() if s == EDGE_FUSE_SLOT else None
+            if s == EDGE_FUSE_SLOT:
+                empty_edge(edge_fuse())
 
             if 0 <= s - 1 < N_MAIN:
                 interleave(s - 1)
@@ -397,7 +409,7 @@ def tile_shiftedpillarsconcatentation_bnact_np9_pa_kernel(tc, xa, W9, b9, Wf, b_
             if s - FUSE_LAG == NP - 1:
                 empty_main(0)
             if s == EDGE_FUSE_SLOT:
-                empty_edge(edge_acc)
+                scatter_edge()
                 store(0)
             if s - FUSE_LAG == N_MAIN - 1:
                 empty_main(1)

@@ -35,6 +35,7 @@ EDGE_PILLARS = [k for k in range(NP) if SHIFTS[k][1] <= 0]
 PILLARS = EDGE_PILLARS + [k for k in range(NP) if SHIFTS[k][1] > 0]
 N_EDGE = len(EDGE_PILLARS)
 N_MAIN = HALVES * NP
+ORDER = (list(range(NP)), list(range(N_EDGE, NP)) + list(range(N_EDGE)))
 
 EDGE_LAG = 3
 FUSE_LAG = 2
@@ -102,11 +103,6 @@ def tile_shiftedpillarsconcatentation_bnact_np9_pa_kernel(tc, xa, W9, b9, Wf, b_
 
         ident = keep.tile([P, P], F32, name="ident")
         make_identity(nc, ident[:])
-
-        bias = keep.tile([P, PACK * (NP + 1)], F32, name="bias")
-        fuse_bias = NP * PACK
-        nc.vector.tensor_copy(out=bias[:, 0:fuse_bias], in_=b9_bf[:].rearrange("p r t -> p (r t)"))
-        nc.vector.tensor_copy(out=bias[:, fuse_bias : fuse_bias + PACK], in_=bf_bf[:])
 
         stage = {}
         for main in (True, False):
@@ -214,7 +210,8 @@ def tile_shiftedpillarsconcatentation_bnact_np9_pa_kernel(tc, xa, W9, b9, Wf, b_
         out_sb = [keep.tile([P, B, PAIR, H * W], F32, name="out_sb%d" % u) for u in range(PAIR)]
 
         def project(n):
-            g, i = divmod(n, NP)
+            g, r = divmod(n, NP)
+            i = ORDER[g][r]
             k = PILLARS[i]
             dh, dw = SHIFTS[k]
             x_lo = X_PAD + g * X_HALF + dw * STRIP
@@ -224,6 +221,7 @@ def tile_shiftedpillarsconcatentation_bnact_np9_pa_kernel(tc, xa, W9, b9, Wf, b_
             span = rows * HALF_B
             planes = flow.tile([P, PACK, MAIN_COLS], BF16, tag="planes", name="planes")
             planes_of[n] = planes
+            left_to_vector = []
             for t in range(PACK):
                 y_ps = work.tile([P, MAIN_COLS], F32, tag="work", name="y_ps")
                 nc.tensor.matmul_mx(
@@ -234,16 +232,17 @@ def tile_shiftedpillarsconcatentation_bnact_np9_pa_kernel(tc, xa, W9, b9, Wf, b_
                     stop=True,
                     **weight_tile("w9", i, t)
                 )
-                nc.scalar.activation(
-                    out=planes[:, t, :].rearrange("p (w s) -> p w s", w=W - 1)[:, first_strip:, dst_lo : dst_lo + span],
-                    in_=y_ps[:].rearrange("p (w s) -> p w s", w=W - 1)[:, first_strip:, src_lo : src_lo + span],
-                    func=IDENTITY,
-                    bias=bias[:, k * PACK + t : k * PACK + t + 1],
-                    scale=1.0,
-                )
+                dst = planes[:, t, :].rearrange("p (w s) -> p w s", w=W - 1)[:, first_strip:, dst_lo : dst_lo + span]
+                src = y_ps[:].rearrange("p (w s) -> p w s", w=W - 1)[:, first_strip:, src_lo : src_lo + span]
+                b_col = b9_bf[:, k, t : t + 1]
+                if n == N_MAIN - 1 and t >= PAIR:
+                    left_to_vector.append((dst, src, b_col))
+                else:
+                    nc.scalar.activation(out=dst, in_=src, func=IDENTITY, bias=b_col, scale=1.0)
+            return left_to_vector
 
         def interleave(n):
-            k = PILLARS[n % NP]
+            k = PILLARS[ORDER[n // NP][n % NP]]
             first_strip, first_row, rows = valid_part(True, k)
             lo = first_row * HALF_B // RUN
             hi = lo + rows * HALF_B // RUN
@@ -253,7 +252,7 @@ def tile_shiftedpillarsconcatentation_bnact_np9_pa_kernel(tc, xa, W9, b9, Wf, b_
             )
 
         def quantise_cat(n):
-            k = PILLARS[n % NP]
+            k = PILLARS[ORDER[n // NP][n % NP]]
             codes = flow.tile([P, MAIN_COLS], U32, tag="cat_codes", name="cat_codes", align_bytes=64)
             scales = flow.tile([P, MAIN_COLS], U8, tag="cat_scales", name="cat_scales", align_bytes=64)
             nc.vector.quantize_mx(
@@ -262,22 +261,23 @@ def tile_shiftedpillarsconcatentation_bnact_np9_pa_kernel(tc, xa, W9, b9, Wf, b_
             cat_of[n] = (codes, scales)
 
         def fuse(n):
-            i = n % NP
+            g, r = divmod(n, NP)
+            i = ORDER[g][r]
             codes, scales = cat_of[n]
             for t in range(PACK):
-                if i == 0:
+                if r == 0:
                     acc_of[t] = accs.tile([P, MAIN_COLS], F32, tag="acc", name="acc")
                 nc.tensor.matmul_mx(
                     out=acc_of[t][:],
                     rhs=codes[:].bitcast(FP8X4),
                     rhs_scale=scales[:],
-                    start=i == 0,
-                    stop=i == NP - 1,
+                    start=r == 0,
+                    stop=r == NP - 1,
                     **weight_tile("wf", i, t)
                 )
 
         def add_fuse_bias(t, dst, src):
-            b_col = bias[:, fuse_bias + t : fuse_bias + t + 1]
+            b_col = bf_bf[:, t : t + 1]
             if t % PAIR == 0:
                 nc.vector.tensor_scalar(out=dst, in0=src, scalar1=b_col, scalar2=None, op0=ADD)
             else:
@@ -331,7 +331,7 @@ def tile_shiftedpillarsconcatentation_bnact_np9_pa_kernel(tc, xa, W9, b9, Wf, b_
             nc.vector.tensor_tensor(
                 out=stage[(False, k)][:, dst_lo : dst_lo + span, :],
                 in0=edge_bank[j][:].rearrange("p t c -> p c t")[:, src_lo : src_lo + span, :],
-                in1=bias[:, k * PACK : (k + 1) * PACK].unsqueeze(1).to_broadcast([P, span, PACK]),
+                in1=b9_bf[:, k, :].unsqueeze(1).to_broadcast([P, span, PACK]),
                 op=ADD,
             )
 
@@ -362,7 +362,7 @@ def tile_shiftedpillarsconcatentation_bnact_np9_pa_kernel(tc, xa, W9, b9, Wf, b_
             nc.vector.tensor_tensor(
                 out=edge_out[:],
                 in0=bank[:],
-                in1=bias[:, fuse_bias : fuse_bias + PACK].unsqueeze(2).to_broadcast([P, PACK, EDGE_COLS]),
+                in1=bf_bf[:].unsqueeze(2).to_broadcast([P, PACK, EDGE_COLS]),
                 op=ADD,
             )
 
@@ -382,12 +382,10 @@ def tile_shiftedpillarsconcatentation_bnact_np9_pa_kernel(tc, xa, W9, b9, Wf, b_
                 regroup_x_main(on_scalar, 0, 5, W - 1)
             if 0 <= j < N_EDGE:
                 edge_project(j)
-            if 0 <= s < N_MAIN:
-                project(s)
+            left_to_vector = project(s) if 0 <= s < N_MAIN else []
             if 0 <= s - FUSE_LAG < N_MAIN:
                 fuse(s - FUSE_LAG)
-            if s == EDGE_FUSE_SLOT:
-                empty_edge(edge_fuse())
+            edge_acc = edge_fuse() if s == EDGE_FUSE_SLOT else None
 
             if 0 <= s - 1 < N_MAIN:
                 interleave(s - 1)
@@ -405,10 +403,14 @@ def tile_shiftedpillarsconcatentation_bnact_np9_pa_kernel(tc, xa, W9, b9, Wf, b_
                 edge_quantise(j - 1)
             for job in x_jobs.get(s, []):
                 job()
+            for dst, src, b_col in left_to_vector:
+                nc.vector.tensor_scalar(out=dst, in0=src, scalar1=b_col, scalar2=None, op0=ADD)
 
             if s - FUSE_LAG == NP - 1:
                 empty_main(0)
             if s == EDGE_FUSE_SLOT:
+                empty_edge(edge_acc)
+            if s == EDGE_FUSE_SLOT + 1:
                 scatter_edge()
                 store(0)
             if s - FUSE_LAG == N_MAIN - 1:

@@ -38,6 +38,7 @@ N_MAIN = HALVES * NP
 ORDER = (list(range(NP)), list(range(N_EDGE, NP)) + list(range(N_EDGE)))
 
 EDGE_LAG = 3
+QUANT_LAG = 1
 FUSE_LAG = 2
 EDGE_FUSE_SLOT = NP + 1
 
@@ -93,10 +94,9 @@ def tile_shiftedpillarsconcatentation_bnact_np9_pa_kernel(tc, xa, W9, b9, Wf, b_
             )
             raw_of[("wf", i)] = wfr
 
+        load_x(0)
         for i in range(NP):
             load_w9(i)
-            if i == 0:
-                load_x(0)
             load_wf(i)
             if i == 2:
                 load_x(1)
@@ -186,7 +186,8 @@ def tile_shiftedpillarsconcatentation_bnact_np9_pa_kernel(tc, xa, W9, b9, Wf, b_
                             words[:, 2 * pair_of_tiles + r, u : PAIR * P : PAIR],
                             ident[:],
                         )
-                nc.scalar.copy(
+                copy = on_vector if (kind == "w9" and i == 0 and pair_of_tiles == 1) else on_scalar
+                copy(
                     out=grouped_words[:, pair_of_tiles * 4 * P : (pair_of_tiles + 1) * 4 * P].rearrange(
                         "p (c u) -> p c u", u=PAIR
                     ),
@@ -221,7 +222,6 @@ def tile_shiftedpillarsconcatentation_bnact_np9_pa_kernel(tc, xa, W9, b9, Wf, b_
             span = rows * HALF_B
             planes = flow.tile([P, PACK, MAIN_COLS], BF16, tag="planes", name="planes")
             planes_of[n] = planes
-            left_to_vector = []
             for t in range(PACK):
                 y_ps = work.tile([P, MAIN_COLS], F32, tag="work", name="y_ps")
                 nc.tensor.matmul_mx(
@@ -232,14 +232,13 @@ def tile_shiftedpillarsconcatentation_bnact_np9_pa_kernel(tc, xa, W9, b9, Wf, b_
                     stop=True,
                     **weight_tile("w9", i, t)
                 )
-                dst = planes[:, t, :].rearrange("p (w s) -> p w s", w=W - 1)[:, first_strip:, dst_lo : dst_lo + span]
-                src = y_ps[:].rearrange("p (w s) -> p w s", w=W - 1)[:, first_strip:, src_lo : src_lo + span]
-                b_col = b9_bf[:, k, t : t + 1]
-                if n == N_MAIN - 1 and t >= PAIR:
-                    left_to_vector.append((dst, src, b_col))
-                else:
-                    nc.scalar.activation(out=dst, in_=src, func=IDENTITY, bias=b_col, scale=1.0)
-            return left_to_vector
+                nc.scalar.activation(
+                    out=planes[:, t, :].rearrange("p (w s) -> p w s", w=W - 1)[:, first_strip:, dst_lo : dst_lo + span],
+                    in_=y_ps[:].rearrange("p (w s) -> p w s", w=W - 1)[:, first_strip:, src_lo : src_lo + span],
+                    func=IDENTITY,
+                    bias=b9_bf[:, k, t : t + 1],
+                    scale=1.0,
+                )
 
         def interleave(n):
             k = PILLARS[ORDER[n // NP][n % NP]]
@@ -253,8 +252,8 @@ def tile_shiftedpillarsconcatentation_bnact_np9_pa_kernel(tc, xa, W9, b9, Wf, b_
 
         def quantise_cat(n):
             k = PILLARS[ORDER[n // NP][n % NP]]
-            codes = flow.tile([P, MAIN_COLS], U32, tag="cat_codes", name="cat_codes", align_bytes=64)
-            scales = flow.tile([P, MAIN_COLS], U8, tag="cat_scales", name="cat_scales", align_bytes=64)
+            codes = flow.tile([P, MAIN_COLS], U32, tag="cat_codes", name="cat_codes", bufs=4, align_bytes=64)
+            scales = flow.tile([P, MAIN_COLS], U8, tag="cat_scales", name="cat_scales", bufs=4, align_bytes=64)
             nc.vector.quantize_mx(
                 out=codes[:].bitcast(FP8X4), scales=scales[:], in_=stage[(True, k)][:].rearrange("p c t -> p (c t)")
             )
@@ -375,14 +374,16 @@ def tile_shiftedpillarsconcatentation_bnact_np9_pa_kernel(tc, xa, W9, b9, Wf, b_
             j = s - EDGE_LAG
             if 0 <= s < NP:
                 transpose_weight("wf", s)
-            if 0 <= s + 1 < NP:
-                transpose_weight("w9", s + 1)
             if s == -1:
                 regroup_x_main(on_vector, 0, 0, 5)
                 regroup_x_main(on_scalar, 0, 5, W - 1)
+                quantise_x(X_PAD, MAIN_COLS)
+            if 0 <= s + 1 < NP:
+                transpose_weight("w9", s + 1)
             if 0 <= j < N_EDGE:
                 edge_project(j)
-            left_to_vector = project(s) if 0 <= s < N_MAIN else []
+            if 0 <= s < N_MAIN:
+                project(s)
             if 0 <= s - FUSE_LAG < N_MAIN:
                 fuse(s - FUSE_LAG)
             edge_acc = edge_fuse() if s == EDGE_FUSE_SLOT else None
@@ -393,18 +394,14 @@ def tile_shiftedpillarsconcatentation_bnact_np9_pa_kernel(tc, xa, W9, b9, Wf, b_
                 quantise_weight("wf", s)
             if 0 <= j < N_EDGE:
                 edge_interleave(j)
-            if 0 <= s - 1 < N_MAIN:
-                quantise_cat(s - 1)
+            if 0 <= s - QUANT_LAG < N_MAIN:
+                quantise_cat(s - QUANT_LAG)
             if 0 <= s + 1 < NP:
                 quantise_weight("w9", s + 1)
-            if s == -1:
-                quantise_x(X_PAD, MAIN_COLS)
             if 0 <= j - 1 < N_EDGE:
                 edge_quantise(j - 1)
             for job in x_jobs.get(s, []):
                 job()
-            for dst, src, b_col in left_to_vector:
-                nc.vector.tensor_scalar(out=dst, in0=src, scalar1=b_col, scalar2=None, op0=ADD)
 
             if s - FUSE_LAG == NP - 1:
                 empty_main(0)

@@ -39,8 +39,8 @@ ORDER = (list(range(NP)), list(range(N_EDGE, NP)) + list(range(N_EDGE)))
 
 EDGE_LAG = 3
 QUANT_LAG = 1
-FUSE_LAG = 2
-EDGE_FUSE_SLOT = NP + 1
+FUSE_LAG = 3
+EDGE_FUSE_SLOT = NP - 1 + FUSE_LAG
 
 
 def valid_part(main, k):
@@ -210,7 +210,7 @@ def tile_shiftedpillarsconcatentation_bnact_np9_pa_kernel(tc, xa, W9, b9, Wf, b_
         acc_of = {}
         out_sb = [keep.tile([P, B, PAIR, H * W], F32, name="out_sb%d" % u) for u in range(PAIR)]
 
-        def project(n):
+        def project(n, t):
             g, r = divmod(n, NP)
             i = ORDER[g][r]
             k = PILLARS[i]
@@ -220,25 +220,25 @@ def tile_shiftedpillarsconcatentation_bnact_np9_pa_kernel(tc, xa, W9, b9, Wf, b_
             dst_lo = first_row * HALF_B
             src_lo = (first_row + dh) * HALF_B
             span = rows * HALF_B
-            planes = flow.tile([P, PACK, MAIN_COLS], BF16, tag="planes", name="planes")
-            planes_of[n] = planes
-            for t in range(PACK):
-                y_ps = work.tile([P, MAIN_COLS], F32, tag="work", name="y_ps")
-                nc.tensor.matmul_mx(
-                    out=y_ps[:],
-                    rhs=x_codes[:, x_lo : x_lo + MAIN_COLS].bitcast(FP8X4),
-                    rhs_scale=x_scales[:, x_lo : x_lo + MAIN_COLS],
-                    start=True,
-                    stop=True,
-                    **weight_tile("w9", i, t)
-                )
-                nc.scalar.activation(
-                    out=planes[:, t, :].rearrange("p (w s) -> p w s", w=W - 1)[:, first_strip:, dst_lo : dst_lo + span],
-                    in_=y_ps[:].rearrange("p (w s) -> p w s", w=W - 1)[:, first_strip:, src_lo : src_lo + span],
-                    func=IDENTITY,
-                    bias=b9_bf[:, k, t : t + 1],
-                    scale=1.0,
-                )
+            if t == 0:
+                planes_of[n] = flow.tile([P, PACK, MAIN_COLS], BF16, tag="planes", name="planes")
+            planes = planes_of[n]
+            y_ps = work.tile([P, MAIN_COLS], F32, tag="work", name="y_ps")
+            nc.tensor.matmul_mx(
+                out=y_ps[:],
+                rhs=x_codes[:, x_lo : x_lo + MAIN_COLS].bitcast(FP8X4),
+                rhs_scale=x_scales[:, x_lo : x_lo + MAIN_COLS],
+                start=True,
+                stop=True,
+                **weight_tile("w9", i, t)
+            )
+            nc.scalar.activation(
+                out=planes[:, t, :].rearrange("p (w s) -> p w s", w=W - 1)[:, first_strip:, dst_lo : dst_lo + span],
+                in_=y_ps[:].rearrange("p (w s) -> p w s", w=W - 1)[:, first_strip:, src_lo : src_lo + span],
+                func=IDENTITY,
+                bias=b9_bf[:, k, t : t + 1],
+                scale=1.0,
+            )
 
         def interleave(n):
             k = PILLARS[ORDER[n // NP][n % NP]]
@@ -259,21 +259,20 @@ def tile_shiftedpillarsconcatentation_bnact_np9_pa_kernel(tc, xa, W9, b9, Wf, b_
             )
             cat_of[n] = (codes, scales)
 
-        def fuse(n):
+        def fuse(n, t):
             g, r = divmod(n, NP)
             i = ORDER[g][r]
             codes, scales = cat_of[n]
-            for t in range(PACK):
-                if r == 0:
-                    acc_of[t] = accs.tile([P, MAIN_COLS], F32, tag="acc", name="acc")
-                nc.tensor.matmul_mx(
-                    out=acc_of[t][:],
-                    rhs=codes[:].bitcast(FP8X4),
-                    rhs_scale=scales[:],
-                    start=r == 0,
-                    stop=r == NP - 1,
-                    **weight_tile("wf", i, t)
-                )
+            if r == 0:
+                acc_of[t] = accs.tile([P, MAIN_COLS], F32, tag="acc", name="acc")
+            nc.tensor.matmul_mx(
+                out=acc_of[t][:],
+                rhs=codes[:].bitcast(FP8X4),
+                rhs_scale=scales[:],
+                start=r == 0,
+                stop=r == NP - 1,
+                **weight_tile("wf", i, t)
+            )
 
         def add_fuse_bias(t, dst, src):
             b_col = bf_bf[:, t : t + 1]
@@ -382,10 +381,11 @@ def tile_shiftedpillarsconcatentation_bnact_np9_pa_kernel(tc, xa, W9, b9, Wf, b_
                 transpose_weight("w9", s + 1)
             if 0 <= j < N_EDGE:
                 edge_project(j)
-            if 0 <= s < N_MAIN:
-                project(s)
-            if 0 <= s - FUSE_LAG < N_MAIN:
-                fuse(s - FUSE_LAG)
+            for t in range(PACK):
+                if 0 <= s < N_MAIN:
+                    project(s, t)
+                if 0 <= s - FUSE_LAG < N_MAIN:
+                    fuse(s - FUSE_LAG, t)
             edge_acc = edge_fuse() if s == EDGE_FUSE_SLOT else None
 
             if 0 <= s - 1 < N_MAIN:

@@ -94,10 +94,11 @@ def tile_shiftedpillarsconcatentation_bnact_np9_pa_kernel(tc, xa, W9, b9, Wf, b_
             )
             raw_of[("wf", i)] = wfr
 
-        load_x(0)
         for i in range(NP):
             load_w9(i)
             load_wf(i)
+            if i == 0:
+                load_x(0)
             if i == 2:
                 load_x(1)
 
@@ -130,17 +131,15 @@ def tile_shiftedpillarsconcatentation_bnact_np9_pa_kernel(tc, xa, W9, b9, Wf, b_
             lo = X_PAD + g * X_HALF
             copy(
                 out=x_grouped[:, lo + w_lo * STRIP : lo + w_hi * STRIP, :].rearrange(
-                    "p (w h b) t -> p w h b t", w=w_hi - w_lo, h=H
+                    "p (w h b) t -> p h b t w", w=w_hi - w_lo, h=H
                 ),
-                in_=x_raw[g][:].rearrange("p b t (h w) -> p w h b t", w=W)[:, w_lo:w_hi],
+                in_=x_raw[g][:].rearrange("p b t (h w) -> p h b t w", w=W)[:, :, :, :, w_lo:w_hi],
             )
 
         def regroup_x_edge(copy, g):
             copy(
-                out=x_grouped[:, X_EDGE:X_COLS, :].rearrange("p (w h g b) t -> p w h g b t", w=2, h=H, g=HALVES)[
-                    :, :, :, g, :, :
-                ],
-                in_=x_raw[g][:].rearrange("p b t (h w) -> p w h b t", w=W)[:, W - 2 : W],
+                out=x_grouped[:, X_EDGE:X_COLS, :].rearrange("p (w h g b) t -> p g h b t w", w=2, h=H, g=HALVES)[:, g],
+                in_=x_raw[g][:].rearrange("p b t (h w) -> p h b t w", w=W)[:, :, :, :, W - 2 : W],
             )
 
         def quantise_x(lo, cols):
@@ -156,9 +155,9 @@ def tile_shiftedpillarsconcatentation_bnact_np9_pa_kernel(tc, xa, W9, b9, Wf, b_
             0: [lambda: regroup_x_main(on_vector, 0, W - 1, W)],
             1: [lambda: quantise_x(X_PAD + MAIN_COLS, STRIP), lambda: regroup_x_edge(on_vector, 0)],
             2: [lambda: regroup_x_edge(on_vector, 1), lambda: quantise_x(X_EDGE, 2 * EDGE_COLS)],
-            3: [lambda: regroup_x_main(on_vector, 1, 0, 3)],
-            4: [lambda: regroup_x_main(on_vector, 1, 3, 6)],
-            5: [lambda: regroup_x_main(on_vector, 1, 6, W)],
+            3: [lambda: regroup_x_main(on_vector, 1, 0, 4)],
+            4: [lambda: regroup_x_main(on_vector, 1, 4, W - 1)],
+            5: [lambda: regroup_x_main(on_vector, 1, W - 1, W)],
             6: [lambda: quantise_x(X_PAD + X_HALF, MAIN_COLS), lambda: quantise_x(X_PAD + X_HALF + MAIN_COLS, STRIP)],
         }
 
@@ -366,19 +365,17 @@ def tile_shiftedpillarsconcatentation_bnact_np9_pa_kernel(tc, xa, W9, b9, Wf, b_
 
         def scatter_edge():
             for t in range(PACK):
-                copy = on_vector if t % PAIR == 0 else on_scalar
-                copy(out=image_of(t)[:, :, :, W - 1], in_=edge_out[:, t, :].rearrange("p (h b) -> p b h", h=H))
+                on_vector(out=image_of(t)[:, :, :, W - 1], in_=edge_out[:, t, :].rearrange("p (h b) -> p b h", h=H))
 
         for s in range(-1, N_MAIN + FUSE_LAG):
             j = s - EDGE_LAG
             if 0 <= s < NP:
                 transpose_weight("wf", s)
-            if s == -1:
-                regroup_x_main(on_vector, 0, 0, 5)
-                regroup_x_main(on_scalar, 0, 5, W - 1)
-                quantise_x(X_PAD, MAIN_COLS)
             if 0 <= s + 1 < NP:
                 transpose_weight("w9", s + 1)
+            if s == -1:
+                regroup_x_main(on_vector, 0, 0, 4)
+                regroup_x_main(on_scalar, 0, 4, W - 1)
             if 0 <= j < N_EDGE:
                 edge_project(j)
             for t in range(PACK):
@@ -398,6 +395,8 @@ def tile_shiftedpillarsconcatentation_bnact_np9_pa_kernel(tc, xa, W9, b9, Wf, b_
                 quantise_cat(s - QUANT_LAG)
             if 0 <= s + 1 < NP:
                 quantise_weight("w9", s + 1)
+            if s == -1:
+                quantise_x(X_PAD, MAIN_COLS)
             if 0 <= j - 1 < N_EDGE:
                 edge_quantise(j - 1)
             for job in x_jobs.get(s, []):

@@ -170,8 +170,10 @@ def tile_shiftedpillarsconcatentation_bnact_np9_pa_kernel(tc, xa, W9, b9, Wf, b_
             "wf": keep.tile([P, NP, C], U8, name="wf_scales", align_bytes=64),
         }
         grouped_of = {}
+        sorted_of = {}
 
         def transpose_weight(kind, i):
+            sorted_words = sorted_of.get((kind, i))
             words = raw_of[(kind, i)][:].bitcast(F32)
             grouped = flow.tile([P, PACK * P * PACK], BF16, tag="w_grouped", name="w_grouped", bufs=4, align_bytes=64)
             grouped_of[(kind, i)] = grouped
@@ -180,9 +182,10 @@ def tile_shiftedpillarsconcatentation_bnact_np9_pa_kernel(tc, xa, W9, b9, Wf, b_
                 bank = work.tile([P, PAIR, 2 * P], F32, tag="work", name="w_bank")
                 for r in range(2):
                     for u in range(PAIR):
+                        row_tile = 2 * pair_of_tiles + r
                         nc.tensor.transpose(
                             bank[:, u, r * P : (r + 1) * P],
-                            words[:, 2 * pair_of_tiles + r, u : PAIR * P : PAIR],
+                            words[:, row_tile, u : PAIR * P : PAIR] if sorted_words is None else sorted_words[:, row_tile, u, :],
                             ident[:],
                         )
                 copy = on_vector if (kind == "w9" and i == 0 and pair_of_tiles == 1) else on_scalar
@@ -192,6 +195,13 @@ def tile_shiftedpillarsconcatentation_bnact_np9_pa_kernel(tc, xa, W9, b9, Wf, b_
                     ),
                     in_=bank[:].rearrange("p u c -> p c u"),
                 )
+
+        def sort_words(kind, i):
+            sorted_words = flow.tile([P, PACK, PAIR, P], F32, tag="w_sorted", name="w_sorted", bufs=3)
+            sorted_of[(kind, i)] = sorted_words
+            nc.vector.tensor_copy(
+                out=sorted_words[:], in_=raw_of[(kind, i)][:].bitcast(F32).rearrange("p t (q u) -> p t u q", u=PAIR)
+            )
 
         def quantise_weight(kind, i):
             nc.vector.quantize_mx(
@@ -401,6 +411,8 @@ def tile_shiftedpillarsconcatentation_bnact_np9_pa_kernel(tc, xa, W9, b9, Wf, b_
                 edge_quantise(j - 1)
             for job in x_jobs.get(s, []):
                 job()
+            if 4 <= s + 3 < NP:
+                sort_words("w9", s + 3)
 
             if s - FUSE_LAG == NP - 1:
                 empty_main(0)

@@ -373,9 +373,8 @@ def tile_shiftedpillarsconcatentation_bnact_np9_pa_kernel(tc, xa, W9, b9, Wf, b_
                 op=ADD,
             )
 
-        def scatter_edge():
-            for t in range(PACK):
-                on_vector(out=image_of(t)[:, :, :, W - 1], in_=edge_out[:, t, :].rearrange("p (h b) -> p b h", h=H))
+        def scatter_edge(t):
+            on_vector(out=image_of(t)[:, :, :, W - 1], in_=edge_out[:, t, :].rearrange("p (h b) -> p b h", h=H))
 
         for s in range(-1, N_MAIN + FUSE_LAG):
             j = s - EDGE_LAG
@@ -418,8 +417,9 @@ def tile_shiftedpillarsconcatentation_bnact_np9_pa_kernel(tc, xa, W9, b9, Wf, b_
                 empty_main(0)
             if s == EDGE_FUSE_SLOT:
                 empty_edge(edge_acc)
-            if s == EDGE_FUSE_SLOT + 1:
-                scatter_edge()
+            if 0 <= s - EDGE_FUSE_SLOT - 1 < PACK:
+                scatter_edge(s - EDGE_FUSE_SLOT - 1)
+            if s == EDGE_FUSE_SLOT + PACK:
                 store(0)
             if s - FUSE_LAG == N_MAIN - 1:
                 empty_main(1)

@@ -37,10 +37,20 @@ N_EDGE = len(EDGE_PILLARS)
 N_MAIN = HALVES * NP
 ORDER = (list(range(NP)), list(range(N_EDGE, NP)) + list(range(N_EDGE)))
 
+VECTOR_BANKS = 2
+EARLY_LAG = 2
 EDGE_LAG = 3
 QUANT_LAG = 1
 FUSE_LAG = 3
-EDGE_FUSE_SLOT = NP - 1 + FUSE_LAG
+EDGE_FUSE_SLOT = NP - 1 + EARLY_LAG
+
+
+def fused_in(s):
+    if 0 <= s - EARLY_LAG < NP:
+        return s - EARLY_LAG
+    if NP <= s - FUSE_LAG < N_MAIN:
+        return s - FUSE_LAG
+    return None
 
 
 def valid_part(main, k):
@@ -170,6 +180,7 @@ def tile_shiftedpillarsconcatentation_bnact_np9_pa_kernel(tc, xa, W9, b9, Wf, b_
             "wf": keep.tile([P, NP, C], U8, name="wf_scales", align_bytes=64),
         }
         grouped_of = {}
+        vector_banks = []
         sorted_of = {}
 
         def transpose_weight(kind, i):
@@ -188,13 +199,18 @@ def tile_shiftedpillarsconcatentation_bnact_np9_pa_kernel(tc, xa, W9, b9, Wf, b_
                             words[:, row_tile, u : PAIR * P : PAIR] if sorted_words is None else sorted_words[:, row_tile, u, :],
                             ident[:],
                         )
-                copy = on_vector if (kind == "w9" and i == 0 and pair_of_tiles == 1) else on_scalar
-                copy(
-                    out=grouped_words[:, pair_of_tiles * 4 * P : (pair_of_tiles + 1) * 4 * P].rearrange(
-                        "p (c u) -> p c u", u=PAIR
-                    ),
-                    in_=bank[:].rearrange("p u c -> p c u"),
-                )
+                def empty(copy, bank=bank, pair_of_tiles=pair_of_tiles):
+                    copy(
+                        out=grouped_words[:, pair_of_tiles * 4 * P : (pair_of_tiles + 1) * 4 * P].rearrange(
+                            "p (c u) -> p c u", u=PAIR
+                        ),
+                        in_=bank[:].rearrange("p u c -> p c u"),
+                    )
+
+                if kind == "w9" and pair_of_tiles == 1 and i <= VECTOR_BANKS:
+                    vector_banks.append(empty)
+                else:
+                    empty(on_scalar)
 
         def sort_words(kind, i):
             sorted_words = flow.tile([P, PACK, PAIR, P], F32, tag="w_sorted", name="w_sorted", bufs=3)
@@ -383,26 +399,30 @@ def tile_shiftedpillarsconcatentation_bnact_np9_pa_kernel(tc, xa, W9, b9, Wf, b_
             if 0 <= s + 1 < NP:
                 transpose_weight("w9", s + 1)
             if s == -1:
+                vector_banks.pop()(on_vector)
+                quantise_weight("w9", 0)
                 regroup_x_main(on_vector, 0, 0, 4)
-                regroup_x_main(on_scalar, 0, 4, W - 1)
+                regroup_x_main(on_vector, 0, 4, W - 1)
             if 0 <= j < N_EDGE:
                 edge_project(j)
             for t in range(PACK):
                 if 0 <= s < N_MAIN:
                     project(s, t)
-                if 0 <= s - FUSE_LAG < N_MAIN:
-                    fuse(s - FUSE_LAG, t)
+                if fused_in(s) is not None:
+                    fuse(fused_in(s), t)
             edge_acc = edge_fuse() if s == EDGE_FUSE_SLOT else None
 
             if 0 <= s - 1 < N_MAIN:
                 interleave(s - 1)
+            if vector_banks:
+                vector_banks.pop()(on_vector)
             if 0 <= s < NP:
                 quantise_weight("wf", s)
             if 0 <= j < N_EDGE:
                 edge_interleave(j)
             if 0 <= s - QUANT_LAG < N_MAIN:
                 quantise_cat(s - QUANT_LAG)
-            if 0 <= s + 1 < NP:
+            if 1 <= s + 1 < NP:
                 quantise_weight("w9", s + 1)
             if s == -1:
                 quantise_x(X_PAD, MAIN_COLS)
@@ -410,10 +430,10 @@ def tile_shiftedpillarsconcatentation_bnact_np9_pa_kernel(tc, xa, W9, b9, Wf, b_
                 edge_quantise(j - 1)
             for job in x_jobs.get(s, []):
                 job()
-            if 4 <= s + 3 < NP:
+            if 6 <= s + 3 < NP:
                 sort_words("w9", s + 3)
 
-            if s - FUSE_LAG == NP - 1:
+            if fused_in(s) == NP - 1:
                 empty_main(0)
             if s == EDGE_FUSE_SLOT:
                 empty_edge(edge_acc)
@@ -421,6 +441,6 @@ def tile_shiftedpillarsconcatentation_bnact_np9_pa_kernel(tc, xa, W9, b9, Wf, b_
                 scatter_edge(s - EDGE_FUSE_SLOT - 1)
             if s == EDGE_FUSE_SLOT + PACK:
                 store(0)
-            if s - FUSE_LAG == N_MAIN - 1:
+            if fused_in(s) == N_MAIN - 1:
                 empty_main(1)
                 store(1)

@@ -400,9 +400,8 @@ def tile_shiftedpillarsconcatentation_bnact_np9_pa_kernel(tc, xa, W9, b9, Wf, b_
                 transpose_weight("w9", s + 1)
             if s == -1:
                 vector_banks.pop()(on_vector)
-                quantise_weight("w9", 0)
                 regroup_x_main(on_vector, 0, 0, 4)
-                regroup_x_main(on_vector, 0, 4, W - 1)
+                regroup_x_main(on_scalar, 0, 4, W - 1)
             if 0 <= j < N_EDGE:
                 edge_project(j)
             for t in range(PACK):
@@ -422,7 +421,7 @@ def tile_shiftedpillarsconcatentation_bnact_np9_pa_kernel(tc, xa, W9, b9, Wf, b_
                 edge_interleave(j)
             if 0 <= s - QUANT_LAG < N_MAIN:
                 quantise_cat(s - QUANT_LAG)
-            if 1 <= s + 1 < NP:
+            if 0 <= s + 1 < NP:
                 quantise_weight("w9", s + 1)
             if s == -1:
                 quantise_x(X_PAD, MAIN_COLS)
@@ -430,7 +429,7 @@ def tile_shiftedpillarsconcatentation_bnact_np9_pa_kernel(tc, xa, W9, b9, Wf, b_
                 edge_quantise(j - 1)
             for job in x_jobs.get(s, []):
                 job()
-            if 6 <= s + 3 < NP:
+            if 5 <= s + 3 < NP:
                 sort_words("w9", s + 3)
 
             if fused_in(s) == NP - 1:

@@ -186,7 +186,7 @@ def tile_shiftedpillarsconcatentation_bnact_np9_pa_kernel(tc, xa, W9, b9, Wf, b_
         def transpose_weight(kind, i):
             sorted_words = sorted_of.get((kind, i))
             words = raw_of[(kind, i)][:].bitcast(F32)
-            grouped = flow.tile([P, PACK * P * PACK], BF16, tag="w_grouped", name="w_grouped", bufs=4, align_bytes=64)
+            grouped = flow.tile([P, PACK * P * PACK], BF16, tag="w_grouped", name="w_grouped", bufs=5, align_bytes=64)
             grouped_of[(kind, i)] = grouped
             grouped_words = grouped[:].bitcast(F32)
             for pair_of_tiles in range(PACK // 2):
@@ -396,6 +396,9 @@ def tile_shiftedpillarsconcatentation_bnact_np9_pa_kernel(tc, xa, W9, b9, Wf, b_
             j = s - EDGE_LAG
             if 0 <= s < NP:
                 transpose_weight("wf", s)
+            early = 2 if fused_in(s) is not None and s < NP - 1 else 0
+            for t in range(early):
+                fuse(fused_in(s), t)
             if 0 <= s + 1 < NP:
                 transpose_weight("w9", s + 1)
             if s == -1:
@@ -404,21 +407,24 @@ def tile_shiftedpillarsconcatentation_bnact_np9_pa_kernel(tc, xa, W9, b9, Wf, b_
                 regroup_x_main(on_scalar, 0, 4, W - 1)
             if 0 <= j < N_EDGE:
                 edge_project(j)
-            for t in range(PACK):
-                if 0 <= s < N_MAIN:
+            if s == N_MAIN - 1:
+                for t in range(PACK):
                     project(s, t)
-                if fused_in(s) is not None:
-                    fuse(fused_in(s), t)
+            for t in range(PACK):
+                if 0 <= s < N_MAIN - 1:
+                    project(s, t)
+                if fused_in(s) is not None and t + early < PACK:
+                    fuse(fused_in(s), t + early)
             edge_acc = edge_fuse() if s == EDGE_FUSE_SLOT else None
 
             if 0 <= s - 1 < N_MAIN:
                 interleave(s - 1)
             if vector_banks:
                 vector_banks.pop()(on_vector)
-            if 0 <= s < NP:
-                quantise_weight("wf", s)
             if 0 <= j < N_EDGE:
                 edge_interleave(j)
+            if 0 <= s < NP:
+                quantise_weight("wf", s)
             if 0 <= s - QUANT_LAG < N_MAIN:
                 quantise_cat(s - QUANT_LAG)
             if 0 <= s + 1 < NP:

@@ -132,8 +132,8 @@ def tile_shiftedpillarsconcatentation_bnact_np9_pa_kernel(tc, xa, W9, b9, Wf, b_
                     nc.gpsimd.memset(view[:, :, empty_row * row : (empty_row + 1) * row, :], 0.0)
 
         x_grouped = keep.tile([P, X_COLS, PACK], BF16, name="x_grouped", align_bytes=64)
-        x_codes = keep.tile([P, X_COLS], U32, name="x_codes", align_bytes=64)
-        x_scales = keep.tile([P, X_COLS], U8, name="x_scales", align_bytes=64)
+        x_codes = keep.tile([P, X_COLS], U32, name="x_codes", align_bytes=256)
+        x_scales = keep.tile([P, X_COLS], U8, name="x_scales", align_bytes=256)
         nc.vector.memset(x_codes[:, 0:X_PAD].bitcast(I32), 0)
         nc.vector.memset(x_scales[:, 0:X_PAD].bitcast(I32), 0)
 
@@ -172,12 +172,12 @@ def tile_shiftedpillarsconcatentation_bnact_np9_pa_kernel(tc, xa, W9, b9, Wf, b_
         }
 
         codes_of = {
-            "w9": keep.tile([P, NP, CO], U32, name="w9_codes", align_bytes=64),
-            "wf": keep.tile([P, NP, C], U32, name="wf_codes", align_bytes=64),
+            "w9": keep.tile([P, NP, CO], U32, name="w9_codes", align_bytes=256),
+            "wf": keep.tile([P, NP, C], U32, name="wf_codes", align_bytes=256),
         }
         scales_of = {
-            "w9": keep.tile([P, NP, CO], U8, name="w9_scales", align_bytes=64),
-            "wf": keep.tile([P, NP, C], U8, name="wf_scales", align_bytes=64),
+            "w9": keep.tile([P, NP, CO], U8, name="w9_scales", align_bytes=256),
+            "wf": keep.tile([P, NP, C], U8, name="wf_scales", align_bytes=256),
         }
         grouped_of = {}
         vector_banks = []
@@ -277,8 +277,8 @@ def tile_shiftedpillarsconcatentation_bnact_np9_pa_kernel(tc, xa, W9, b9, Wf, b_
 
         def quantise_cat(n):
             k = PILLARS[ORDER[n // NP][n % NP]]
-            codes = flow.tile([P, MAIN_COLS], U32, tag="cat_codes", name="cat_codes", bufs=4, align_bytes=64)
-            scales = flow.tile([P, MAIN_COLS], U8, tag="cat_scales", name="cat_scales", bufs=4, align_bytes=64)
+            codes = flow.tile([P, MAIN_COLS], U32, tag="cat_codes", name="cat_codes", bufs=4, align_bytes=256)
+            scales = flow.tile([P, MAIN_COLS], U8, tag="cat_scales", name="cat_scales", bufs=4, align_bytes=256)
             nc.vector.quantize_mx(
                 out=codes[:].bitcast(FP8X4), scales=scales[:], in_=stage[(True, k)][:].rearrange("p c t -> p (c t)")
             )
@@ -327,8 +327,8 @@ def tile_shiftedpillarsconcatentation_bnact_np9_pa_kernel(tc, xa, W9, b9, Wf, b_
                     in_=out_sb[u][:, g * HALF_B : (g + 1) * HALF_B].rearrange("p b e s -> p b (e s)"),
                 )
 
-        edge_codes = keep.tile([P, N_EDGE, EDGE_COLS], U32, name="edge_codes", align_bytes=64)
-        edge_scales = keep.tile([P, N_EDGE, EDGE_COLS], U8, name="edge_scales", align_bytes=64)
+        edge_codes = keep.tile([P, N_EDGE, EDGE_COLS], U32, name="edge_codes", align_bytes=256)
+        edge_scales = keep.tile([P, N_EDGE, EDGE_COLS], U8, name="edge_scales", align_bytes=256)
         edge_bank = {}
 
         def edge_project(j):
@@ -435,7 +435,7 @@ def tile_shiftedpillarsconcatentation_bnact_np9_pa_kernel(tc, xa, W9, b9, Wf, b_
                 edge_quantise(j - 1)
             for job in x_jobs.get(s, []):
                 job()
-            if 5 <= s + 3 < NP:
+            if 4 <= s + 3 < NP:
                 sort_words("w9", s + 3)
 
             if fused_in(s) == NP - 1:

@@ -70,10 +70,13 @@ def tile_shiftedpillarsconcatentation_bnact_np9_pa_kernel(tc, xa, W9, b9, Wf, b_
         accs = stack.enter_context(tc.psum_pool(name="accs", bufs=PACK))
         stack.enter_context(tc.manual_schedule())
 
-        b9_bf = keep.tile([P, NP, PACK], BF16, name="b9_bf")
-        nc.scalar.dma_start(out=b9_bf[:], in_=b9.rearrange("k (p t) -> p k t", t=PACK))
-        bf_bf = keep.tile([P, PACK], BF16, name="bf_bf")
-        nc.scalar.dma_start(out=bf_bf[:], in_=b_fuse.rearrange("(p t) -> p t", t=PACK))
+        bias_rows = keep.tile([P, CO], BF16, name="bias_rows")
+        nc.vector.memset(bias_rows[:], 0.0)
+        nc.scalar.dma_start(out=bias_rows[0:NP, :], in_=b9)
+        nc.scalar.dma_start(out=bias_rows[NP : NP + 1, :], in_=b_fuse.rearrange("(k o) -> k o", k=1))
+        biases = keep.tile([P, NP + 1, PACK], BF16, name="biases")
+        b9_bf = biases[:, 0:NP, :]
+        bf_bf = biases[:, NP, :]
 
         x_raw = {}
         raw_of = {}
@@ -211,6 +214,16 @@ def tile_shiftedpillarsconcatentation_bnact_np9_pa_kernel(tc, xa, W9, b9, Wf, b_
                     vector_banks.append(empty)
                 else:
                     empty(on_scalar)
+
+        def transpose_biases():
+            words = bias_rows[:].bitcast(F32)
+            bank = work.tile([P, PAIR, P], F32, tag="work", name="bias_bank")
+            for u in range(PAIR):
+                nc.tensor.transpose(bank[:, u, :], words[:, u : PAIR * P : PAIR], ident[:])
+            nc.vector.tensor_copy(
+                out=biases[:].rearrange("p k t -> p (k t)").bitcast(F32).rearrange("p (k u) -> p k u", u=PAIR),
+                in_=bank[:, :, 0 : NP + 1].rearrange("p u k -> p k u"),
+            )
 
         def sort_words(kind, i):
             sorted_words = flow.tile([P, PACK, PAIR, P], F32, tag="w_sorted", name="w_sorted", bufs=3)
@@ -403,6 +416,7 @@ def tile_shiftedpillarsconcatentation_bnact_np9_pa_kernel(tc, xa, W9, b9, Wf, b_
                 transpose_weight("w9", s + 1)
             if s == -1:
                 vector_banks.pop()(on_vector)
+                transpose_biases()
                 regroup_x_main(on_vector, 0, 0, 4)
                 regroup_x_main(on_scalar, 0, 4, W - 1)
             if 0 <= j < N_EDGE:

@@ -72,8 +72,12 @@ def tile_shiftedpillarsconcatentation_bnact_np9_pa_kernel(tc, xa, W9, b9, Wf, b_
 
         bias_rows = keep.tile([P, CO], BF16, name="bias_rows")
         nc.vector.memset(bias_rows[:], 0.0)
-        nc.scalar.dma_start(out=bias_rows[0:NP, :], in_=b9)
-        nc.scalar.dma_start(out=bias_rows[NP : NP + 1, :], in_=b_fuse.rearrange("(k o) -> k o", k=1))
+
+        def load_biases():
+            nc.sync.dma_start(out=bias_rows[0 : NP - 1, :], in_=b9[0 : NP - 1])
+            nc.sync.dma_start(out=bias_rows[NP - 1 : NP, :], in_=b9[NP - 1 : NP])
+            nc.sync.dma_start(out=bias_rows[NP : NP + 1, :], in_=b_fuse.rearrange("(k o) -> k o", k=1))
+
         biases = keep.tile([P, NP + 1, PACK], BF16, name="biases")
         b9_bf = biases[:, 0:NP, :]
         bf_bf = biases[:, NP, :]
@@ -109,9 +113,10 @@ def tile_shiftedpillarsconcatentation_bnact_np9_pa_kernel(tc, xa, W9, b9, Wf, b_
 
         for i in range(NP):
             load_w9(i)
-            load_wf(i)
             if i == 0:
                 load_x(0)
+                load_biases()
+            load_wf(i)
             if i == 2:
                 load_x(1)
 
@@ -414,9 +419,10 @@ def tile_shiftedpillarsconcatentation_bnact_np9_pa_kernel(tc, xa, W9, b9, Wf, b_
                 fuse(fused_in(s), t)
             if 0 <= s + 1 < NP:
                 transpose_weight("w9", s + 1)
+            if s == 0:
+                transpose_biases()
             if s == -1:
                 vector_banks.pop()(on_vector)
-                transpose_biases()
                 regroup_x_main(on_vector, 0, 0, 4)
                 regroup_x_main(on_scalar, 0, 4, W - 1)
             if 0 <= j < N_EDGE:

from contextlib import ExitStack

import concourse.mybir as mybir
from concourse.masks import make_identity

F32 = mybir.dt.float32
BF16 = mybir.dt.bfloat16
I32 = mybir.dt.int32
U32 = mybir.dt.uint32
U8 = mybir.dt.uint8
FP8X4 = mybir.dt.float8_e4m3fn_x4
IDENTITY = mybir.ActivationFunctionType.Identity
ADD = mybir.AluOpType.add

B, C, H, W, NP, CO = 16, 512, 8, 9, 9, 512
SHIFTS = ((0, 0), (0, 0), (0, 0), (0, -1), (0, 1), (1, -1), (1, 1), (-1, -1), (-1, 1))
USED = sum((H - abs(dh)) * (W - abs(dw)) for dh, dw in SHIFTS)
FLOPS = 2 * NP * CO * C * B * H * W + 2 * C * CO * B * USED

P = 128
PACK = 4
PAIR = 2
HALVES = 2
HALF_B = B // HALVES
STRIP = H * HALF_B
MAIN_COLS = (W - 1) * STRIP
EDGE_COLS = H * B
X_PAD = STRIP
X_HALF = W * STRIP
X_EDGE = X_PAD + HALVES * X_HALF
X_COLS = X_EDGE + 2 * EDGE_COLS
RUN = 4

EDGE_PILLARS = [k for k in range(NP) if SHIFTS[k][1] <= 0]
PILLARS = EDGE_PILLARS + [k for k in range(NP) if SHIFTS[k][1] > 0]
N_EDGE = len(EDGE_PILLARS)
N_MAIN = HALVES * NP
ORDER = (list(range(NP)), list(range(N_EDGE, NP)) + list(range(N_EDGE)))

VECTOR_BANKS = 2
EARLY_LAG = 2
EDGE_LAG = 3
QUANT_LAG = 1
FUSE_LAG = 3
EDGE_FUSE_SLOT = NP - 1 + EARLY_LAG


def fused_in(s):
    if 0 <= s - EARLY_LAG < NP:
        return s - EARLY_LAG
    if NP <= s - FUSE_LAG < N_MAIN:
        return s - FUSE_LAG
    return None


def valid_part(main, k):
    dh, dw = SHIFTS[k]
    first_strip = 1 if (main and dw < 0) else 0
    return first_strip, max(-dh, 0), H - abs(dh)


def tile_shiftedpillarsconcatentation_bnact_np9_pa_kernel(tc, xa, W9, b9, Wf, b_fuse, out):
    nc = tc.nc

    with ExitStack() as stack:
        keep = stack.enter_context(tc.tile_pool(name="keep", bufs=1))
        raw_pool = stack.enter_context(tc.tile_pool(name="raw", bufs=4))
        flow = stack.enter_context(tc.tile_pool(name="flow", bufs=3))
        work = stack.enter_context(tc.psum_pool(name="work", bufs=4))
        accs = stack.enter_context(tc.psum_pool(name="accs", bufs=PACK))
        stack.enter_context(tc.manual_schedule())

        bias_rows = keep.tile([P, CO], BF16, name="bias_rows")
        nc.vector.memset(bias_rows[:], 0.0)

        def load_biases():
            nc.sync.dma_start(out=bias_rows[0 : NP - 1, :], in_=b9[0 : NP - 1])
            nc.sync.dma_start(out=bias_rows[NP - 1 : NP, :], in_=b9[NP - 1 : NP])
            nc.sync.dma_start(out=bias_rows[NP : NP + 1, :], in_=b_fuse.rearrange("(k o) -> k o", k=1))

        biases = keep.tile([P, NP + 1, PACK], BF16, name="biases")
        b9_bf = biases[:, 0:NP, :]
        bf_bf = biases[:, NP, :]

        x_raw = {}
        raw_of = {}

        def load_x(g):
            xr = keep.tile([P, HALF_B, PACK, H * W], BF16, name="x_raw%d" % g)
            nc.sync.dma_start(
                out=xr[:].rearrange("p b t s -> p b (t s)"),
                in_=xa[g * HALF_B : (g + 1) * HALF_B].rearrange("b (p t) h w -> p b (t h w)", t=PACK),
            )
            x_raw[g] = xr

        def load_w9(i):
            k = PILLARS[i]
            w9r = raw_pool.tile([P, PACK, C], BF16, tag="w9_raw", name="w9_raw%d" % k)
            nc.sync.dma_start(
                out=w9r[:].rearrange("p t c -> p (t c)"),
                in_=W9[k].rearrange("(p t) c -> p (t c)", t=PACK),
            )
            raw_of[("w9", i)] = w9r

        def load_wf(i):
            k = PILLARS[i]
            wfr = raw_pool.tile([P, PACK, CO], BF16, tag="wf_raw", name="wf_raw%d" % k)
            nc.sync.dma_start(
                out=wfr[:],
                in_=Wf[:, k * CO : (k + 1) * CO].rearrange("(p t) j -> p t j", t=PACK),
            )
            raw_of[("wf", i)] = wfr

        for i in range(NP):
            load_w9(i)
            if i == 0:
                load_x(0)
                load_biases()
            load_wf(i)
            if i == 2:
                load_x(1)

        ident = keep.tile([P, P], F32, name="ident")
        make_identity(nc, ident[:])

        stage = {}
        for main in (True, False):
            strips, strip_cols, row = (W - 1, STRIP, HALF_B) if main else (1, EDGE_COLS, B)
            for k in PILLARS if main else EDGE_PILLARS:
                st = keep.tile(
                    [P, strips * strip_cols, PACK], BF16, name="stage%d_%d" % (strip_cols, k), align_bytes=64
                )
                stage[(main, k)] = st
                first_strip, first_row, rows = valid_part(main, k)
                view = st[:].rearrange("p (w s) t -> p w s t", w=strips)
                if first_strip:
                    nc.gpsimd.memset(view[:, 0:first_strip], 0.0)
                if rows < H:
                    empty_row = 0 if first_row else H - 1
                    nc.gpsimd.memset(view[:, :, empty_row * row : (empty_row + 1) * row, :], 0.0)

        x_grouped = keep.tile([P, X_COLS, PACK], BF16, name="x_grouped", align_bytes=64)
        x_codes = keep.tile([P, X_COLS], U32, name="x_codes", align_bytes=256)
        x_scales = keep.tile([P, X_COLS], U8, name="x_scales", align_bytes=256)
        nc.vector.memset(x_codes[:, 0:X_PAD].bitcast(I32), 0)
        nc.vector.memset(x_scales[:, 0:X_PAD].bitcast(I32), 0)

        def regroup_x_main(copy, g, w_lo, w_hi):
            lo = X_PAD + g * X_HALF
            copy(
                out=x_grouped[:, lo + w_lo * STRIP : lo + w_hi * STRIP, :].rearrange(
                    "p (w h b) t -> p h b t w", w=w_hi - w_lo, h=H
                ),
                in_=x_raw[g][:].rearrange("p b t (h w) -> p h b t w", w=W)[:, :, :, :, w_lo:w_hi],
            )

        def regroup_x_edge(copy, g):
            copy(
                out=x_grouped[:, X_EDGE:X_COLS, :].rearrange("p (w h g b) t -> p g h b t w", w=2, h=H, g=HALVES)[:, g],
                in_=x_raw[g][:].rearrange("p b t (h w) -> p h b t w", w=W)[:, :, :, :, W - 2 : W],
            )

        def quantise_x(lo, cols):
            nc.vector.quantize_mx(
                out=x_codes[:, lo : lo + cols].bitcast(FP8X4),
                scales=x_scales[:, lo : lo + cols],
                in_=x_grouped[:, lo : lo + cols, :].rearrange("p c t -> p (c t)"),
            )

        on_vector = nc.vector.tensor_copy
        on_scalar = nc.scalar.copy
        x_jobs = {
            0: [lambda: regroup_x_main(on_vector, 0, W - 1, W)],
            1: [lambda: quantise_x(X_PAD + MAIN_COLS, STRIP), lambda: regroup_x_edge(on_vector, 0)],
            2: [lambda: regroup_x_edge(on_vector, 1), lambda: quantise_x(X_EDGE, 2 * EDGE_COLS)],
            3: [lambda: regroup_x_main(on_vector, 1, 0, 4)],
            4: [lambda: regroup_x_main(on_vector, 1, 4, W - 1)],
            5: [lambda: regroup_x_main(on_vector, 1, W - 1, W)],
            6: [lambda: quantise_x(X_PAD + X_HALF, MAIN_COLS), lambda: quantise_x(X_PAD + X_HALF + MAIN_COLS, STRIP)],
        }

        codes_of = {
            "w9": keep.tile([P, NP, CO], U32, name="w9_codes", align_bytes=256),
            "wf": keep.tile([P, NP, C], U32, name="wf_codes", align_bytes=256),
        }
        scales_of = {
            "w9": keep.tile([P, NP, CO], U8, name="w9_scales", align_bytes=256),
            "wf": keep.tile([P, NP, C], U8, name="wf_scales", align_bytes=256),
        }
        grouped_of = {}
        vector_banks = []
        sorted_of = {}

        def transpose_weight(kind, i):
            sorted_words = sorted_of.get((kind, i))
            words = raw_of[(kind, i)][:].bitcast(F32)
            grouped = flow.tile([P, PACK * P * PACK], BF16, tag="w_grouped", name="w_grouped", bufs=5, align_bytes=64)
            grouped_of[(kind, i)] = grouped
            grouped_words = grouped[:].bitcast(F32)
            for pair_of_tiles in range(PACK // 2):
                bank = work.tile([P, PAIR, 2 * P], F32, tag="work", name="w_bank")
                for r in range(2):
                    for u in range(PAIR):
                        row_tile = 2 * pair_of_tiles + r
                        nc.tensor.transpose(
                            bank[:, u, r * P : (r + 1) * P],
                            words[:, row_tile, u : PAIR * P : PAIR] if sorted_words is None else sorted_words[:, row_tile, u, :],
                            ident[:],
                        )
                def empty(copy, bank=bank, pair_of_tiles=pair_of_tiles):
                    copy(
                        out=grouped_words[:, pair_of_tiles * 4 * P : (pair_of_tiles + 1) * 4 * P].rearrange(
                            "p (c u) -> p c u", u=PAIR
                        ),
                        in_=bank[:].rearrange("p u c -> p c u"),
                    )

                if kind == "w9" and pair_of_tiles == 1 and i <= VECTOR_BANKS:
                    vector_banks.append(empty)
                else:
                    empty(on_scalar)

        def transpose_biases():
            words = bias_rows[:].bitcast(F32)
            bank = work.tile([P, PAIR, P], F32, tag="work", name="bias_bank")
            for u in range(PAIR):
                nc.tensor.transpose(bank[:, u, :], words[:, u : PAIR * P : PAIR], ident[:])
            nc.vector.tensor_copy(
                out=biases[:].rearrange("p k t -> p (k t)").bitcast(F32).rearrange("p (k u) -> p k u", u=PAIR),
                in_=bank[:, :, 0 : NP + 1].rearrange("p u k -> p k u"),
            )

        def sort_words(kind, i):
            sorted_words = flow.tile([P, PACK, PAIR, P], F32, tag="w_sorted", name="w_sorted", bufs=3)
            sorted_of[(kind, i)] = sorted_words
            nc.vector.tensor_copy(
                out=sorted_words[:], in_=raw_of[(kind, i)][:].bitcast(F32).rearrange("p t (q u) -> p t u q", u=PAIR)
            )

        def quantise_weight(kind, i):
            nc.vector.quantize_mx(
                out=codes_of[kind][:, i, :].bitcast(FP8X4), scales=scales_of[kind][:, i, :], in_=grouped_of[(kind, i)][:]
            )

        def weight_tile(kind, i, t):
            return dict(
                lhsT=codes_of[kind][:, i, t * P : (t + 1) * P].bitcast(FP8X4),
                lhsT_scale=scales_of[kind][:, i, t * P : (t + 1) * P],
            )

        planes_of = {}
        cat_of = {}
        acc_of = {}
        out_sb = [keep.tile([P, B, PAIR, H * W], F32, name="out_sb%d" % u) for u in range(PAIR)]

        def project(n, t):
            g, r = divmod(n, NP)
            i = ORDER[g][r]
            k = PILLARS[i]
            dh, dw = SHIFTS[k]
            x_lo = X_PAD + g * X_HALF + dw * STRIP
            first_strip, first_row, rows = valid_part(True, k)
            dst_lo = first_row * HALF_B
            src_lo = (first_row + dh) * HALF_B
            span = rows * HALF_B
            if t == 0:
                planes_of[n] = flow.tile([P, PACK, MAIN_COLS], BF16, tag="planes", name="planes")
            planes = planes_of[n]
            y_ps = work.tile([P, MAIN_COLS], F32, tag="work", name="y_ps")
            nc.tensor.matmul_mx(
                out=y_ps[:],
                rhs=x_codes[:, x_lo : x_lo + MAIN_COLS].bitcast(FP8X4),
                rhs_scale=x_scales[:, x_lo : x_lo + MAIN_COLS],
                start=True,
                stop=True,
                **weight_tile("w9", i, t)
            )
            nc.scalar.activation(
                out=planes[:, t, :].rearrange("p (w s) -> p w s", w=W - 1)[:, first_strip:, dst_lo : dst_lo + span],
                in_=y_ps[:].rearrange("p (w s) -> p w s", w=W - 1)[:, first_strip:, src_lo : src_lo + span],
                func=IDENTITY,
                bias=b9_bf[:, k, t : t + 1],
                scale=1.0,
            )

        def interleave(n):
            k = PILLARS[ORDER[n // NP][n % NP]]
            first_strip, first_row, rows = valid_part(True, k)
            lo = first_row * HALF_B // RUN
            hi = lo + rows * HALF_B // RUN
            nc.vector.tensor_copy(
                out=stage[(True, k)][:].rearrange("p (w c r) t -> p w c t r", w=W - 1, r=RUN)[:, first_strip:, lo:hi],
                in_=planes_of[n][:].rearrange("p t (w c r) -> p w c t r", w=W - 1, r=RUN)[:, first_strip:, lo:hi],
            )

        def quantise_cat(n):
            k = PILLARS[ORDER[n // NP][n % NP]]
            codes = flow.tile([P, MAIN_COLS], U32, tag="cat_codes", name="cat_codes", bufs=4, align_bytes=256)
            scales = flow.tile([P, MAIN_COLS], U8, tag="cat_scales", name="cat_scales", bufs=4, align_bytes=256)
            nc.vector.quantize_mx(
                out=codes[:].bitcast(FP8X4), scales=scales[:], in_=stage[(True, k)][:].rearrange("p c t -> p (c t)")
            )
            cat_of[n] = (codes, scales)

        def fuse(n, t):
            g, r = divmod(n, NP)
            i = ORDER[g][r]
            codes, scales = cat_of[n]
            if r == 0:
                acc_of[t] = accs.tile([P, MAIN_COLS], F32, tag="acc", name="acc")
            nc.tensor.matmul_mx(
                out=acc_of[t][:],
                rhs=codes[:].bitcast(FP8X4),
                rhs_scale=scales[:],
                start=r == 0,
                stop=r == NP - 1,
                **weight_tile("wf", i, t)
            )

        def add_fuse_bias(t, dst, src):
            b_col = bf_bf[:, t : t + 1]
            if t % PAIR == 0:
                nc.vector.tensor_scalar(out=dst, in0=src, scalar1=b_col, scalar2=None, op0=ADD)
            else:
                nc.scalar.activation(out=dst, in_=src, func=IDENTITY, bias=b_col, scale=1.0)

        def image_of(t):
            u, e = divmod(t, PAIR)
            return out_sb[u][:, :, e, :].rearrange("p b (h w) -> p b h w", w=W)

        def empty_main(g):
            for t in range(PACK):
                add_fuse_bias(
                    t,
                    image_of(t)[:, g * HALF_B : (g + 1) * HALF_B, :, 0 : W - 1],
                    acc_of[t][:].rearrange("p (w h b) -> p b h w", w=W - 1, h=H),
                )

        def store(g):
            for u in range(PAIR):
                nc.sync.dma_start(
                    out=out[g * HALF_B : (g + 1) * HALF_B].rearrange(
                        "b (p u e) h w -> u p b (e h w)", u=PAIR, e=PAIR
                    )[u],
                    in_=out_sb[u][:, g * HALF_B : (g + 1) * HALF_B].rearrange("p b e s -> p b (e s)"),
                )

        edge_codes = keep.tile([P, N_EDGE, EDGE_COLS], U32, name="edge_codes", align_bytes=256)
        edge_scales = keep.tile([P, N_EDGE, EDGE_COLS], U8, name="edge_scales", align_bytes=256)
        edge_bank = {}

        def edge_project(j):
            x_lo = X_EDGE + EDGE_COLS + SHIFTS[PILLARS[j]][1] * EDGE_COLS
            y_bank = work.tile([P, PACK, EDGE_COLS], F32, tag="work", name="y_bank")
            edge_bank[j] = y_bank
            for t in range(PACK):
                nc.tensor.matmul_mx(
                    out=y_bank[:, t, :],
                    rhs=x_codes[:, x_lo : x_lo + EDGE_COLS].bitcast(FP8X4),
                    rhs_scale=x_scales[:, x_lo : x_lo + EDGE_COLS],
                    start=True,
                    stop=True,
                    **weight_tile("w9", j, t)
                )

        def edge_interleave(j):
            k = PILLARS[j]
            first_strip, first_row, rows = valid_part(False, k)
            dst_lo = first_row * B
            src_lo = (first_row + SHIFTS[k][0]) * B
            span = rows * B
            nc.vector.tensor_tensor(
                out=stage[(False, k)][:, dst_lo : dst_lo + span, :],
                in0=edge_bank[j][:].rearrange("p t c -> p c t")[:, src_lo : src_lo + span, :],
                in1=b9_bf[:, k, :].unsqueeze(1).to_broadcast([P, span, PACK]),
                op=ADD,
            )

        def edge_quantise(j):
            nc.vector.quantize_mx(
                out=edge_codes[:, j, :].bitcast(FP8X4),
                scales=edge_scales[:, j, :],
                in_=stage[(False, PILLARS[j])][:].rearrange("p c t -> p (c t)"),
            )

        def edge_fuse():
            bank = work.tile([P, PACK, EDGE_COLS], F32, tag="work", name="edge_acc")
            for t in range(PACK):
                for j in range(N_EDGE):
                    nc.tensor.matmul_mx(
                        out=bank[:, t, :],
                        rhs=edge_codes[:, j, :].bitcast(FP8X4),
                        rhs_scale=edge_scales[:, j, :],
                        start=j == 0,
                        stop=j == N_EDGE - 1,
                        **weight_tile("wf", j, t)
                    )
            return bank

        edge_out = keep.tile([P, PACK, EDGE_COLS], F32, name="edge_out")

        def empty_edge(bank):
            nc.vector.tensor_tensor(
                out=edge_out[:],
                in0=bank[:],
                in1=bf_bf[:].unsqueeze(2).to_broadcast([P, PACK, EDGE_COLS]),
                op=ADD,
            )

        def scatter_edge(t):
            on_vector(out=image_of(t)[:, :, :, W - 1], in_=edge_out[:, t, :].rearrange("p (h b) -> p b h", h=H))

        for s in range(-1, N_MAIN + FUSE_LAG):
            j = s - EDGE_LAG
            if 0 <= s < NP:
                transpose_weight("wf", s)
            early = 2 if fused_in(s) is not None and s < NP - 1 else 0
            for t in range(early):
                fuse(fused_in(s), t)
            if 0 <= s + 1 < NP:
                transpose_weight("w9", s + 1)
            if s == 0:
                transpose_biases()
            if s == -1:
                vector_banks.pop()(on_vector)
                regroup_x_main(on_vector, 0, 0, 4)
                regroup_x_main(on_scalar, 0, 4, W - 1)
            if 0 <= j < N_EDGE:
                edge_project(j)
            if s == N_MAIN - 1:
                for t in range(PACK):
                    project(s, t)
            for t in range(PACK):
                if 0 <= s < N_MAIN - 1:
                    project(s, t)
                if fused_in(s) is not None and t + early < PACK:
                    fuse(fused_in(s), t + early)
            edge_acc = edge_fuse() if s == EDGE_FUSE_SLOT else None

            if 0 <= s - 1 < N_MAIN:
                interleave(s - 1)
            if vector_banks:
                vector_banks.pop()(on_vector)
            if 0 <= j < N_EDGE:
                edge_interleave(j)
            if 0 <= s < NP:
                quantise_weight("wf", s)
            if 0 <= s - QUANT_LAG < N_MAIN:
                quantise_cat(s - QUANT_LAG)
            if 0 <= s + 1 < NP:
                quantise_weight("w9", s + 1)
            if s == -1:
                quantise_x(X_PAD, MAIN_COLS)
            if 0 <= j - 1 < N_EDGE:
                edge_quantise(j - 1)
            for job in x_jobs.get(s, []):
                job()
            if 4 <= s + 3 < NP:
                sort_words("w9", s + 3)

            if fused_in(s) == NP - 1:
                empty_main(0)
            if s == EDGE_FUSE_SLOT:
                empty_edge(edge_acc)
            if 0 <= s - EDGE_FUSE_SLOT - 1 < PACK:
                scatter_edge(s - EDGE_FUSE_SLOT - 1)
            if s == EDGE_FUSE_SLOT + PACK:
                store(0)
            if fused_in(s) == N_MAIN - 1:
                empty_main(1)
                store(1)
